import numpy as np
import ml_dtypes


def mxq(x, axis, fmt="e4m3"):
    dtype, down = {"e4m3": (ml_dtypes.float8_e4m3fn, 7), "e5m2": (ml_dtypes.float8_e5m2, 14)}[fmt]
    v = np.moveaxis(np.asarray(x, np.float32).astype(ml_dtypes.bfloat16).astype(np.float64), axis, -1)
    blocks = v.reshape(v.shape[:-1] + (-1, 32))
    amax = np.abs(blocks).max(-1, keepdims=True)
    byte = np.maximum(np.where(amax > 0, np.frexp(amax)[1] - 1 + 127, 0) - down, 1)
    scale = np.exp2(byte - 127.0)
    codes = (blocks / scale).astype(np.float32).astype(dtype).astype(np.float64)
    return np.moveaxis((codes * scale).reshape(v.shape), -1, axis)


WIDE = False


def mx_kscale(k):
    if not WIDE:
        return np.ones(k)
    levels = np.array([20, -20, 10, -10, 0])
    a = np.random.permutation(np.resize(levels, k // 512 * 4)).reshape(k // 512, 4)
    idx = np.arange(k)
    return np.exp2(a[idx // 512, idx % 128 // 32])


BF16 = ml_dtypes.bfloat16


def bf(x):
    return np.asarray(x, np.float32).astype(BF16)


def f64(x):
    return np.asarray(x).astype(np.float64)


B, I, O, G = 8192, 128, 512, 5
DEGREE = 3
NB = G + DEGREE
GRID_MIN, GRID_MAX = -1.0, 1.0


def extended_grid():
    h = (GRID_MAX - GRID_MIN) / G
    return GRID_MIN + h * np.arange(-DEGREE, G + DEGREE + 1).astype(np.float64)


def bspline(u, degree):
    t = extended_grid()
    G0 = G + 2 * DEGREE
    ue = u[..., None]
    n = ((ue >= t[:-1]) & (ue < t[1:])).astype(np.float64)
    for k in range(1, degree + 1):
        cnt = G0 - k
        left = (ue - t[:cnt]) / (t[k:k + cnt] - t[:cnt])
        right = (t[k + 1:k + 1 + cnt] - ue) / (t[k + 1:k + 1 + cnt] - t[1:1 + cnt])
        n = left * n[..., :-1] + right * n[..., 1:]
    return n


def bspline_slope(u):
    t = extended_grid()
    n2 = bspline(u, DEGREE - 1)
    return DEGREE * (n2[..., :-1] / (t[DEGREE:DEGREE + NB] - t[:NB])
                     - n2[..., 1:] / (t[DEGREE + 1:DEGREE + 1 + NB] - t[1:1 + NB]))


def setup_inputs():
    u = mx_kscale(O)
    x = f64(bf(np.random.standard_normal((B, I))))
    x = np.where(np.abs(x) == 1.0, 0.5 * x, x)
    c = np.random.standard_normal((O, I, NB)) * 2.0 / np.sqrt(I) / u[:, None, None]
    w = np.random.standard_normal((O, I)) / np.sqrt(I) / u[:, None]
    b = np.random.standard_normal(O) * 0.3
    sb = np.random.uniform(0.5, 1.5, (O, 1)) + 0.3 * np.random.standard_normal((O, I))
    g = np.random.standard_normal((B, O)) * np.exp2(np.random.randint(-12, 1, (B, 1))) * 4.0 * u[None, :]
    return {"x": bf(x), "spline_coeffs": bf(c), "residual_weight": bf(w), "residual_bias": bf(b),
            "scale_base": bf(sb), "grad_out": bf(g)}


def reference(x, spline_coeffs, residual_weight, residual_bias, scale_base, grad_out):
    x = f64(x)
    g = f64(grad_out)
    scale = np.mean(f64(scale_base), axis=1)
    gs = g * scale[None, :]
    d = (mxq(gs, 1, "e5m2") @ mxq(f64(spline_coeffs).reshape(O, I * NB), 0, "e4m3")).reshape(B, I, NB)
    r = mxq(g, 1, "e5m2") @ mxq(f64(residual_weight), 0, "e4m3")
    inside = ((x > GRID_MIN) & (x < GRID_MAX)).astype(np.float64)
    slope = bspline_slope(np.clip(x, GRID_MIN, GRID_MAX))
    return inside * np.sum(slope * d, axis=2) + r

@@ -1,0 +1,219 @@
+from contextlib import ExitStack
+import math
+
+import concourse.mybir as mybir
+from concourse.masks import make_identity
+
+F32 = mybir.dt.float32
+BF16 = mybir.dt.bfloat16
+U32 = mybir.dt.uint32
+U8 = mybir.dt.uint8
+E4X4 = mybir.dt.float8_e4m3fn_x4
+E5X4 = mybir.dt.float8_e5m2_x4
+ALU = mybir.AluOpType
+ACT = mybir.ActivationFunctionType
+AX = mybir.AxisListType
+
+P = 128
+B, I, O, NB = 8192, 128, 512, 8
+NT = B // P
+CH = 4
+CT = CH * P
+NCH = NT // CH
+FLOPS = 2 * B * O * (I * NB + I)
+
+H = 0.4
+INV_H = 2.5
+ALPHA = math.sqrt(0.5 * INV_H)
+BETA = math.sqrt(INV_H)
+
+
+def tile_bsplinebasis_t_kernel(tc, x, spline_coeffs, residual_weight, residual_bias, scale_base, grad_out, out):
+    nc = tc.nc
+    g_view = grad_out.rearrange("(p n) o -> p n o", n=NT)
+    x_view = x.rearrange("(p n) i -> p n i", n=NT)
+    o_view = out.rearrange("(p n) i -> p n i", n=NT)
+    c_flat = spline_coeffs.rearrange("o i j -> o (i j)")
+
+    with ExitStack() as ctx:
+        const = ctx.enter_context(tc.tile_pool(name="const", bufs=1))
+        setup = ctx.enter_context(tc.tile_pool(name="setup", bufs=1))
+        gin = ctx.enter_context(tc.tile_pool(name="gin", bufs=3))
+        gq_pool = ctx.enter_context(tc.tile_pool(name="gq", bufs=2))
+        basis = ctx.enter_context(tc.tile_pool(name="basis", bufs=2))
+        work = ctx.enter_context(tc.tile_pool(name="work", bufs=2))
+        prods = ctx.enter_context(tc.tile_pool(name="prods", bufs=4))
+        ps_e = ctx.enter_context(tc.psum_pool(name="ps_e", bufs=4))
+        ps_a = ctx.enter_context(tc.psum_pool(name="ps_a", bufs=1))
+        ps_t = ctx.enter_context(tc.psum_pool(name="ps_t", bufs=2))
+
+        ident_f = const.tile([P, P], F32)
+        make_identity(nc, ident_f[:])
+        ident_b = const.tile([P, P], BF16)
+        make_identity(nc, ident_b[:])
+
+        sbraw = setup.tile([P, 4, I], BF16)
+        for u in range(2):
+            nc.sync.dma_start(out=sbraw[:, 2 * u:2 * u + 2, :],
+                              in_=scale_base[256 * u:256 * u + 256, :].rearrange("(q e) c -> q e c", e=2))
+        g_tiles = {}
+
+        def load_g(c):
+            g_sb = gin.tile([P, CH, O], BF16, name="g_sb")
+            nc.sync.dma_start(out=g_sb[:], in_=g_view[:, CH * c:CH * c + CH, :])
+            g_tiles[c] = g_sb
+
+        load_g(0)
+        craw = setup.tile([P, 4, I * NB], BF16)
+        for u in range(2):
+            nc.sync.dma_start(out=craw[:, 2 * u:2 * u + 2, :],
+                              in_=c_flat[256 * u:256 * u + 256, :].rearrange("(q e) c -> q e c", e=2))
+        wraw = setup.tile([P, 4, I], BF16)
+        for u in range(2):
+            nc.sync.dma_start(out=wraw[:, 2 * u:2 * u + 2, :],
+                              in_=residual_weight[256 * u:256 * u + 256, :].rearrange("(q e) c -> q e c", e=2))
+        x_sb = const.tile([P, NT, I], BF16)
+        nc.sync.dma_start(out=x_sb[:], in_=x_view)
+        load_g(1)
+
+        ssum = setup.tile([P, 4], F32)
+        nc.vector.tensor_reduce(out=ssum[:], in_=sbraw[:], axis=AX.X, op=ALU.add)
+        scale4 = const.tile([P, 4], F32)
+        nc.vector.tensor_scalar(out=scale4[:], in0=ssum[:], scalar1=1.0 / I, scalar2=None, op0=ALU.mult)
+        scale_b = scale4[:].rearrange("p (u e) -> p u e", e=2).unsqueeze(1).to_broadcast([P, 2 * P, 2, 2])
+
+        cgp = setup.tile([P, NB, I, 4], BF16, align_bytes=64)
+        cgn = setup.tile([P, NB, I, 4], BF16, align_bytes=64)
+        c_perm = craw[:].rearrange("p t (i j) -> p j i t", j=NB)
+        cp_codes = const.tile([P, NB * I], U32, align_bytes=64)
+        cp_scl = const.tile([P, NB * I], U8, align_bytes=64)
+        cn_codes = const.tile([P, NB * I], U32, align_bytes=64)
+        cn_scl = const.tile([P, NB * I], U8, align_bytes=64)
+        nc.vector.tensor_copy(out=cgp[:, 0:4], in_=c_perm[:, 0:4])
+        nc.scalar.mul(out=cgn[:, 0:4], in_=c_perm[:, 0:4], mul=-1.0)
+        nc.vector.tensor_copy(out=cgp[:, 4:8], in_=c_perm[:, 4:8])
+        nc.gpsimd.tensor_scalar(out=cgn[:, 4:8], in0=c_perm[:, 4:8], scalar1=-1.0, scalar2=0.0, op0=ALU.mult, op1=ALU.add)
+        wg = setup.tile([P, I, 4], BF16, align_bytes=64)
+        nc.vector.tensor_copy(out=wg[:], in_=wraw[:].rearrange("p t i -> p i t"))
+        w_codes = const.tile([P, I], U32, align_bytes=64)
+        w_scl = const.tile([P, I], U8, align_bytes=64)
+        for hf in range(2):
+            cols = slice(512 * hf, 512 * hf + 512)
+            nc.vector.quantize_mx(out=cp_codes[:, cols].bitcast(E4X4), scales=cp_scl[:, cols],
+                                  in_=cgp[:, 4 * hf:4 * hf + 4].rearrange("p j i t -> p (j i t)"))
+            nc.vector.quantize_mx(out=cn_codes[:, cols].bitcast(E4X4), scales=cn_scl[:, cols],
+                                  in_=cgn[:, 4 * hf:4 * hf + 4].rearrange("p j i t -> p (j i t)"))
+        nc.vector.quantize_mx(out=w_codes[:].bitcast(E4X4), scales=w_scl[:], in_=wg[:].rearrange("p i t -> p (i t)"))
+
+        xT = const.tile([P, B], BF16)
+        for grp in range(NT // 8):
+            xt_ps = ps_t.tile([P, 8 * P], BF16, tag="tr")
+            for k in range(8):
+                nc.tensor.transpose(xt_ps[:, P * k:P * k + P], x_sb[:, 8 * grp + k, :], ident_b[:])
+            nc.scalar.copy(out=xT[:, 1024 * grp:1024 * grp + 1024], in_=xt_ps[:])
+        a_nat = const.tile([P, NT, I], BF16)
+        for q in range(4):
+            nc.scalar.activation(out=a_nat[:, 16 * q:16 * q + 16, :], in_=x_sb[:, 16 * q:16 * q + 16, :], func=ACT.Abs)
+
+        q_tiles = {}
+
+        def prep_g(c):
+            g_sb = g_tiles.pop(c)
+            gq = gq_pool.tile([P, CT, 4], BF16, name="gq", align_bytes=64)
+            gsq = gq_pool.tile([P, CT, 4], BF16, name="gsq", align_bytes=64)
+            for hf in range(2):
+                bank = ps_t.tile([P, 2, 2 * P], F32, tag="tr")
+                for k in range(2):
+                    gw = g_sb[:, 2 * hf + k, :].bitcast(F32)
+                    for u in range(2):
+                        nc.tensor.transpose(bank[:, u, P * k:P * k + P], gw[:, P * u:P * u + P], ident_f[:])
+                toks = slice(256 * hf, 256 * hf + 256)
+                nc.scalar.copy(out=gq[:, toks, :].bitcast(F32), in_=bank[:].rearrange("p u t -> p t u"))
+                nc.vector.tensor_tensor(out=gsq[:, toks, :].rearrange("p t (u e) -> p t u e", e=2),
+                                        in0=bank[:].bitcast(BF16).rearrange("p u (t e) -> p t u e", e=2),
+                                        in1=scale_b, op=ALU.mult)
+            g_codes = gq_pool.tile([P, CT], U32, name="g_codes", align_bytes=64)
+            g_scl = gq_pool.tile([P, CT], U8, name="g_scl", align_bytes=64)
+            gs_codes = gq_pool.tile([P, CT], U32, name="gs_codes", align_bytes=64)
+            gs_scl = gq_pool.tile([P, CT], U8, name="gs_scl", align_bytes=64)
+            nc.vector.quantize_mx(out=gs_codes[:].bitcast(E5X4), scales=gs_scl[:], in_=gsq[:].rearrange("p t k -> p (t k)"))
+            nc.vector.quantize_mx(out=g_codes[:].bitcast(E5X4), scales=g_scl[:], in_=gq[:].rearrange("p t k -> p (t k)"))
+            q_tiles[c] = (g_codes, g_scl, gs_codes, gs_scl)
+
+        plane_tiles = {}
+
+        def prep_basis(c):
+            xs = xT[:, CT * c:CT * c + CT]
+            z = []
+            for k in range(5):
+                zk = basis.tile([P, CT], F32, name="z%d" % k)
+                nc.gpsimd.tensor_scalar(out=zk[:], in0=xs, scalar1=-1.0 + H * (k + 1), scalar2=-1.0 + H * k,
+                                        op0=ALU.min, op1=ALU.max)
+                z.append(zk)
+            planes = {}
+            p1 = basis.tile([P, CT], F32, name="pl1")
+            nc.scalar.activation(out=p1[:], in_=z[0][:], func=ACT.Square, scale=-INV_H * ALPHA, bias=-1.5 * ALPHA)
+            planes[1] = p1
+            p7 = basis.tile([P, CT], F32, name="pl7")
+            nc.scalar.activation(out=p7[:], in_=z[4][:], func=ACT.Square, scale=INV_H * ALPHA, bias=-1.5 * ALPHA)
+            planes[7] = p7
+            for j in range(2, 7):
+                xj = basis.tile([P, CT], F32, name="pl%d" % j)
+                if j == 2:
+                    nc.scalar.activation(out=xj[:], in_=z[1][:], func=ACT.Square, scale=-INV_H * ALPHA, bias=-0.5 * ALPHA)
+                elif j == 6:
+                    nc.scalar.activation(out=xj[:], in_=z[3][:], func=ACT.Square, scale=INV_H * ALPHA, bias=-0.5 * ALPHA)
+                else:
+                    dz = basis.tile([P, CT], F32, name="dz%d" % j)
+                    nc.gpsimd.tensor_tensor(out=dz[:], in0=z[j - 3][:], in1=z[j - 1][:], op=ALU.subtract)
+                    nc.scalar.activation(out=xj[:], in_=dz[:], func=ACT.Square, scale=INV_H * ALPHA, bias=2.0 * ALPHA)
+                k = j - 2
+                sq = basis.tile([P, CT], F32, name="sq%d" % k)
+                nc.scalar.activation(out=sq[:], in_=z[k][:], func=ACT.Square, scale=INV_H * BETA, bias=(2.0 - k) * BETA)
+                nc.gpsimd.tensor_tensor(out=xj[:], in0=xj[:], in1=sq[:], op=ALU.subtract)
+                planes[j] = xj
+            plane_tiles[c] = planes
+
+        def main(c):
+            g_codes, g_scl, gs_codes, gs_scl = q_tiles.pop(c)
+            planes = plane_tiles.pop(c)
+            acc = ps_a.tile([P, CH, I], F32, name="acc")
+            accr = ps_a.tile([P, CH, I], F32, name="accr")
+            e_r = ps_e.tile([P, CT], F32, tag="e")
+            nc.tensor.matmul_mx(out=e_r[:], lhsT=w_codes[:].bitcast(E4X4), lhsT_scale=w_scl[:],
+                                rhs=g_codes[:].bitcast(E5X4), rhs_scale=g_scl[:], start=True, stop=True)
+            r_t = work.tile([P, CT], F32, name="r_t")
+            nc.scalar.copy(out=r_t[:], in_=e_r[:])
+            for j in range(1, 8):
+                e_j = ps_e.tile([P, CT], F32, tag="e")
+                nc.tensor.matmul_mx(out=e_j[:], lhsT=cp_codes[:, I * j:I * j + I].bitcast(E4X4),
+                                    lhsT_scale=cp_scl[:, I * j:I * j + I],
+                                    rhs=gs_codes[:].bitcast(E5X4), rhs_scale=gs_scl[:], start=True, stop=False)
+                nc.tensor.matmul_mx(out=e_j[:], lhsT=cn_codes[:, I * (j - 1):I * j].bitcast(E4X4),
+                                    lhsT_scale=cn_scl[:, I * (j - 1):I * j],
+                                    rhs=gs_codes[:].bitcast(E5X4), rhs_scale=gs_scl[:], start=False, stop=True)
+                pr = prods.tile([P, CT], F32, name="pr")
+                shift = 0.0 if j in (1, 7) else 0.25 * INV_H
+                nc.vector.scalar_tensor_tensor(out=pr[:], in0=planes[j][:], scalar=shift, in1=e_j[:],
+                                               op0=ALU.add, op1=ALU.mult)
+                for n in range(CH):
+                    nc.tensor.matmul(out=acc[:, n, :], lhsT=pr[:, P * n:P * n + P], rhs=ident_f[:], is_transpose=True,
+                                     start=(j == 1 and n == 0), stop=(j == 7 and n == CH - 1))
+            for n in range(CH):
+                nc.tensor.transpose(accr[:, n, :], r_t[:, P * n:P * n + P], ident_f[:])
+            tmp = work.tile([P, CH, I], F32, name="tmp")
+            nc.vector.scalar_tensor_tensor(out=tmp[:], in0=a_nat[:, CH * c:CH * c + CH, :], scalar=1.0, in1=acc[:],
+                                           op0=ALU.is_lt, op1=ALU.mult)
+            o_sb = work.tile([P, CH, I], F32, name="o_sb")
+            nc.vector.tensor_tensor(out=o_sb[:], in0=tmp[:], in1=accr[:], op=ALU.add)
+            nc.sync.dma_start(out=o_view[:, CH * c:CH * c + CH, :], in_=o_sb[:])
+
+        prep_g(0)
+        prep_basis(0)
+        for c in range(NCH):
+            if c + 2 < NCH:
+                load_g(c + 2)
+            if c + 1 < NCH:
+                prep_g(c + 1)
+                prep_basis(c + 1)
+            main(c)

@@ -25,7 +25,7 @@ FLOPS = 2 * B * O * (I * NB + I)
 H = 0.4
 INV_H = 2.5
 ALPHA = math.sqrt(0.5 * INV_H)
-BETA = math.sqrt(INV_H)
+PIN = False
 
 
 def tile_bsplinebasis_t_kernel(tc, x, spline_coeffs, residual_weight, residual_bias, scale_base, grad_out, out):
@@ -42,7 +42,7 @@ def tile_bsplinebasis_t_kernel(tc, x, spline_coeffs, residual_weight, residual_b
         gq_pool = ctx.enter_context(tc.tile_pool(name="gq", bufs=2))
         basis = ctx.enter_context(tc.tile_pool(name="basis", bufs=2))
         work = ctx.enter_context(tc.tile_pool(name="work", bufs=2))
-        prods = ctx.enter_context(tc.tile_pool(name="prods", bufs=4))
+        prods = ctx.enter_context(tc.tile_pool(name="prods", bufs=10))
         ps_e = ctx.enter_context(tc.psum_pool(name="ps_e", bufs=4))
         ps_a = ctx.enter_context(tc.psum_pool(name="ps_a", bufs=1))
         ps_t = ctx.enter_context(tc.psum_pool(name="ps_t", bufs=2))
@@ -73,7 +73,8 @@ def tile_bsplinebasis_t_kernel(tc, x, spline_coeffs, residual_weight, residual_b
             nc.sync.dma_start(out=wraw[:, 2 * u:2 * u + 2, :],
                               in_=residual_weight[256 * u:256 * u + 256, :].rearrange("(q e) c -> q e c", e=2))
         x_sb = const.tile([P, NT, I], BF16)
-        nc.sync.dma_start(out=x_sb[:], in_=x_view)
+        nc.sync.dma_start(out=x_sb[:, 0:16, :], in_=x_view[:, 0:16, :])
+        nc.sync.dma_start(out=x_sb[:, 16:NT, :], in_=x_view[:, 16:NT, :])
         load_g(1)
 
         ssum = setup.tile([P, 4], F32)
@@ -90,9 +91,13 @@ def tile_bsplinebasis_t_kernel(tc, x, spline_coeffs, residual_weight, residual_b
         cn_codes = const.tile([P, NB * I], U32, align_bytes=64)
         cn_scl = const.tile([P, NB * I], U8, align_bytes=64)
         nc.vector.tensor_copy(out=cgp[:, 0:4], in_=c_perm[:, 0:4])
-        nc.scalar.mul(out=cgn[:, 0:4], in_=c_perm[:, 0:4], mul=-1.0)
+        nc.scalar.mul(out=cgn[:, 0:4], in_=c_perm[:, 0:4], mul=-2.0)
         nc.vector.tensor_copy(out=cgp[:, 4:8], in_=c_perm[:, 4:8])
-        nc.gpsimd.tensor_scalar(out=cgn[:, 4:8], in0=c_perm[:, 4:8], scalar1=-1.0, scalar2=0.0, op0=ALU.mult, op1=ALU.add)
+        nc.gpsimd.tensor_scalar(out=cgn[:, 4:8], in0=c_perm[:, 4:8], scalar1=-2.0, scalar2=0.0, op0=ALU.mult, op1=ALU.add)
+        cg1 = setup.tile([P, I, 4], BF16, align_bytes=64)
+        nc.scalar.mul(out=cg1[:], in_=c_perm[:, 1], mul=-1.0)
+        c1_codes = const.tile([P, I], U32, align_bytes=64)
+        c1_scl = const.tile([P, I], U8, align_bytes=64)
         wg = setup.tile([P, I, 4], BF16, align_bytes=64)
         nc.vector.tensor_copy(out=wg[:], in_=wraw[:].rearrange("p t i -> p i t"))
         w_codes = const.tile([P, I], U32, align_bytes=64)
@@ -104,16 +109,17 @@ def tile_bsplinebasis_t_kernel(tc, x, spline_coeffs, residual_weight, residual_b
             nc.vector.quantize_mx(out=cn_codes[:, cols].bitcast(E4X4), scales=cn_scl[:, cols],
                                   in_=cgn[:, 4 * hf:4 * hf + 4].rearrange("p j i t -> p (j i t)"))
         nc.vector.quantize_mx(out=w_codes[:].bitcast(E4X4), scales=w_scl[:], in_=wg[:].rearrange("p i t -> p (i t)"))
+        nc.vector.quantize_mx(out=c1_codes[:].bitcast(E4X4), scales=c1_scl[:], in_=cg1[:].rearrange("p i t -> p (i t)"))
 
         xT = const.tile([P, B], BF16)
-        for grp in range(NT // 8):
+        a_nat = const.tile([P, NT, I], BF16)
+
+        def prep_x(grp):
             xt_ps = ps_t.tile([P, 8 * P], BF16, tag="tr")
             for k in range(8):
                 nc.tensor.transpose(xt_ps[:, P * k:P * k + P], x_sb[:, 8 * grp + k, :], ident_b[:])
             nc.scalar.copy(out=xT[:, 1024 * grp:1024 * grp + 1024], in_=xt_ps[:])
-        a_nat = const.tile([P, NT, I], BF16)
-        for q in range(4):
-            nc.scalar.activation(out=a_nat[:, 16 * q:16 * q + 16, :], in_=x_sb[:, 16 * q:16 * q + 16, :], func=ACT.Abs)
+            nc.scalar.activation(out=a_nat[:, 8 * grp:8 * grp + 8, :], in_=x_sb[:, 8 * grp:8 * grp + 8, :], func=ACT.Abs)
 
         q_tiles = {}
 
@@ -121,17 +127,25 @@ def tile_bsplinebasis_t_kernel(tc, x, spline_coeffs, residual_weight, residual_b
             g_sb = g_tiles.pop(c)
             gq = gq_pool.tile([P, CT, 4], BF16, name="gq", align_bytes=64)
             gsq = gq_pool.tile([P, CT, 4], BF16, name="gsq", align_bytes=64)
+            banks = []
             for hf in range(2):
                 bank = ps_t.tile([P, 2, 2 * P], F32, tag="tr")
                 for k in range(2):
                     gw = g_sb[:, 2 * hf + k, :].bitcast(F32)
                     for u in range(2):
                         nc.tensor.transpose(bank[:, u, P * k:P * k + P], gw[:, P * u:P * u + P], ident_f[:])
+                banks.append(bank)
+            for hf in range(2):
+                bank = banks[hf]
                 toks = slice(256 * hf, 256 * hf + 256)
-                nc.scalar.copy(out=gq[:, toks, :].bitcast(F32), in_=bank[:].rearrange("p u t -> p t u"))
                 nc.vector.tensor_tensor(out=gsq[:, toks, :].rearrange("p t (u e) -> p t u e", e=2),
                                         in0=bank[:].bitcast(BF16).rearrange("p u (t e) -> p t u e", e=2),
                                         in1=scale_b, op=ALU.mult)
+                nc.scalar.copy(out=gq[:, toks, :].bitcast(F32), in_=bank[:].rearrange("p u t -> p t u"))
+            q_tiles[c] = (gq, gsq)
+
+        def quant_g(c):
+            gq, gsq = q_tiles.pop(c)
             g_codes = gq_pool.tile([P, CT], U32, name="g_codes", align_bytes=64)
             g_scl = gq_pool.tile([P, CT], U8, name="g_scl", align_bytes=64)
             gs_codes = gq_pool.tile([P, CT], U32, name="gs_codes", align_bytes=64)
@@ -143,64 +157,97 @@ def tile_bsplinebasis_t_kernel(tc, x, spline_coeffs, residual_weight, residual_b
         plane_tiles = {}
 
         def prep_basis(c):
-            xs = xT[:, CT * c:CT * c + CT]
+            ws = xT[:, CT * c:CT * c + CT]
             z = []
             for k in range(5):
                 zk = basis.tile([P, CT], F32, name="z%d" % k)
-                nc.gpsimd.tensor_scalar(out=zk[:], in0=xs, scalar1=-1.0 + H * (k + 1), scalar2=-1.0 + H * k,
+                nc.gpsimd.tensor_scalar(out=zk[:], in0=ws, scalar1=-1.0 + H * (k + 1), scalar2=-1.0 + H * k,
                                         op0=ALU.min, op1=ALU.max)
                 z.append(zk)
-            planes = {}
-            p1 = basis.tile([P, CT], F32, name="pl1")
-            nc.scalar.activation(out=p1[:], in_=z[0][:], func=ACT.Square, scale=-INV_H * ALPHA, bias=-1.5 * ALPHA)
-            planes[1] = p1
-            p7 = basis.tile([P, CT], F32, name="pl7")
-            nc.scalar.activation(out=p7[:], in_=z[4][:], func=ACT.Square, scale=INV_H * ALPHA, bias=-1.5 * ALPHA)
-            planes[7] = p7
-            for j in range(2, 7):
-                xj = basis.tile([P, CT], F32, name="pl%d" % j)
-                if j == 2:
-                    nc.scalar.activation(out=xj[:], in_=z[1][:], func=ACT.Square, scale=-INV_H * ALPHA, bias=-0.5 * ALPHA)
-                elif j == 6:
-                    nc.scalar.activation(out=xj[:], in_=z[3][:], func=ACT.Square, scale=INV_H * ALPHA, bias=-0.5 * ALPHA)
-                else:
-                    dz = basis.tile([P, CT], F32, name="dz%d" % j)
-                    nc.gpsimd.tensor_tensor(out=dz[:], in0=z[j - 3][:], in1=z[j - 1][:], op=ALU.subtract)
-                    nc.scalar.activation(out=xj[:], in_=dz[:], func=ACT.Square, scale=INV_H * ALPHA, bias=2.0 * ALPHA)
-                k = j - 2
-                sq = basis.tile([P, CT], F32, name="sq%d" % k)
-                nc.scalar.activation(out=sq[:], in_=z[k][:], func=ACT.Square, scale=INV_H * BETA, bias=(2.0 - k) * BETA)
-                nc.gpsimd.tensor_tensor(out=xj[:], in0=xj[:], in1=sq[:], op=ALU.subtract)
-                planes[j] = xj
+            up = []
+            dn = []
+            for k in range(5):
+                dk = basis.tile([P, CT], F32, name="dn%d" % k)
+                nc.scalar.activation(out=dk[:], in_=z[k][:], func=ACT.Square, scale=-INV_H * ALPHA, bias=(k - 1.5) * ALPHA)
+                dn.append(dk)
+                uk = basis.tile([P, CT], F32, name="up%d" % k)
+                nc.scalar.activation(out=uk[:], in_=z[k][:], func=ACT.Square, scale=INV_H * ALPHA, bias=(2.5 - k) * ALPHA)
+                up.append(uk)
+            planes = {-1: dn[0], 4: up[4]}
+            for a in range(4):
+                eng = nc.vector if a < 2 else nc.gpsimd
+                eng.tensor_tensor(out=up[a][:], in0=up[a][:], in1=dn[a + 1][:], op=ALU.subtract)
+                planes[a] = up[a]
             plane_tiles[c] = planes
 
-        def main(c):
+        def pos(j):
+            return cp_codes[:, I * j:I * j + I].bitcast(E4X4), cp_scl[:, I * j:I * j + I]
+
+        def neg2(j):
+            return cn_codes[:, I * j:I * j + I].bitcast(E4X4), cn_scl[:, I * j:I * j + I]
+
+        def group(ops, rhs, rhs_scl):
+            e_j = ps_e.tile([P, CT], F32, tag="e")
+            for idx, (cd, sc) in enumerate(ops):
+                nc.tensor.matmul_mx(out=e_j[:], lhsT=cd, lhsT_scale=sc, rhs=rhs[:].bitcast(E5X4), rhs_scale=rhs_scl[:],
+                                    start=(idx == 0), stop=(idx == len(ops) - 1))
+            return e_j
+
+        acc_tiles = {}
+        pending = {}
+
+        def mx_first(c):
+            g_codes, g_scl, gs_codes, gs_scl = q_tiles[c]
+            planes = plane_tiles[c]
+            e_r = group([(w_codes[:].bitcast(E4X4), w_scl[:])], g_codes, g_scl)
+            e_c = group([pos(2), (c1_codes[:].bitcast(E4X4), c1_scl[:])], gs_codes, gs_scl)
+            e_m = group([pos(2), neg2(1), pos(0)], gs_codes, gs_scl)
+            e_0 = group([pos(3), neg2(2), pos(1)], gs_codes, gs_scl)
+            out_list = []
+            pr = prods.tile([P, CT], F32, name="pr")
+            nc.scalar.copy(out=pr[:], in_=e_r[:])
+            out_list.append(pr)
+            pr = prods.tile([P, CT], F32, name="pr")
+            nc.scalar.mul(out=pr[:], in_=e_c[:], mul=INV_H)
+            out_list.append(pr)
+            pr = prods.tile([P, CT], F32, name="pr")
+            nc.vector.scalar_tensor_tensor(out=pr[:], in0=planes[-1][:], scalar=-1.0, in1=e_m[:], op0=ALU.mult, op1=ALU.mult)
+            out_list.append(pr)
+            pr = prods.tile([P, CT], F32, name="pr")
+            nc.vector.scalar_tensor_tensor(out=pr[:], in0=planes[0][:], scalar=0.5 * INV_H, in1=e_0[:], op0=ALU.add, op1=ALU.mult)
+            out_list.append(pr)
+            pending[(c, 0)] = out_list
+
+        def mx_second(c):
             g_codes, g_scl, gs_codes, gs_scl = q_tiles.pop(c)
             planes = plane_tiles.pop(c)
+            banks = [group([pos(a + 3), neg2(a + 2), pos(a + 1)], gs_codes, gs_scl) for a in range(1, 5)]
+            out_list = []
+            for a in range(1, 5):
+                pr = prods.tile([P, CT], F32, name="pr")
+                nc.vector.scalar_tensor_tensor(out=pr[:], in0=planes[a][:], scalar=(0.0 if a == 4 else 0.5 * INV_H), in1=banks[a - 1][:],
+                                               op0=ALU.add, op1=ALU.mult)
+                out_list.append(pr)
+            pending[(c, 1)] = out_list
+
+        def acc_first(c):
             acc = ps_a.tile([P, CH, I], F32, name="acc")
             accr = ps_a.tile([P, CH, I], F32, name="accr")
-            e_r = ps_e.tile([P, CT], F32, tag="e")
-            nc.tensor.matmul_mx(out=e_r[:], lhsT=w_codes[:].bitcast(E4X4), lhsT_scale=w_scl[:],
-                                rhs=g_codes[:].bitcast(E5X4), rhs_scale=g_scl[:], start=True, stop=True)
-            r_t = work.tile([P, CT], F32, name="r_t")
-            nc.scalar.copy(out=r_t[:], in_=e_r[:])
-            for j in range(1, 8):
-                e_j = ps_e.tile([P, CT], F32, tag="e")
-                nc.tensor.matmul_mx(out=e_j[:], lhsT=cp_codes[:, I * j:I * j + I].bitcast(E4X4),
-                                    lhsT_scale=cp_scl[:, I * j:I * j + I],
-                                    rhs=gs_codes[:].bitcast(E5X4), rhs_scale=gs_scl[:], start=True, stop=False)
-                nc.tensor.matmul_mx(out=e_j[:], lhsT=cn_codes[:, I * (j - 1):I * j].bitcast(E4X4),
-                                    lhsT_scale=cn_scl[:, I * (j - 1):I * j],
-                                    rhs=gs_codes[:].bitcast(E5X4), rhs_scale=gs_scl[:], start=False, stop=True)
-                pr = prods.tile([P, CT], F32, name="pr")
-                shift = 0.0 if j in (1, 7) else 0.25 * INV_H
-                nc.vector.scalar_tensor_tensor(out=pr[:], in0=planes[j][:], scalar=shift, in1=e_j[:],
-                                               op0=ALU.add, op1=ALU.mult)
+            acc_tiles[c] = (acc, accr)
+            plist = pending.pop((c, 0))
+            for n in range(CH):
+                nc.tensor.transpose(accr[:, n, :], plist[0][:, P * n:P * n + P], ident_f[:])
+            for idx, pr in enumerate(plist[1:]):
                 for n in range(CH):
                     nc.tensor.matmul(out=acc[:, n, :], lhsT=pr[:, P * n:P * n + P], rhs=ident_f[:], is_transpose=True,
-                                     start=(j == 1 and n == 0), stop=(j == 7 and n == CH - 1))
-            for n in range(CH):
-                nc.tensor.transpose(accr[:, n, :], r_t[:, P * n:P * n + P], ident_f[:])
+                                     start=(idx == 0 and n == 0), stop=False)
+
+        def acc_second(c):
+            acc, accr = acc_tiles.pop(c)
+            for idx, pr in enumerate(pending.pop((c, 1))):
+                for n in range(CH):
+                    nc.tensor.matmul(out=acc[:, n, :], lhsT=pr[:, P * n:P * n + P], rhs=ident_f[:], is_transpose=True,
+                                     start=False, stop=(idx == 3 and n == CH - 1))
             tmp = work.tile([P, CH, I], F32, name="tmp")
             nc.vector.scalar_tensor_tensor(out=tmp[:], in0=a_nat[:, CH * c:CH * c + CH, :], scalar=1.0, in1=acc[:],
                                            op0=ALU.is_lt, op1=ALU.mult)
@@ -208,12 +255,25 @@ def tile_bsplinebasis_t_kernel(tc, x, spline_coeffs, residual_weight, residual_b
             nc.vector.tensor_tensor(out=o_sb[:], in0=tmp[:], in1=accr[:], op=ALU.add)
             nc.sync.dma_start(out=o_view[:, CH * c:CH * c + CH, :], in_=o_sb[:])
 
+        if PIN:
+            ctx.enter_context(tc.manual_schedule())
+        prep_x(0)
         prep_g(0)
         prep_basis(0)
+        quant_g(0)
         for c in range(NCH):
             if c + 2 < NCH:
                 load_g(c + 2)
+            mx_first(c)
             if c + 1 < NCH:
                 prep_g(c + 1)
+            if c % 2 == 0 and c // 2 + 1 < NT // 8:
+                prep_x(c // 2 + 1)
+            if c > 0:
+                acc_second(c - 1)
+            mx_second(c)
+            if c + 1 < NCH:
+                quant_g(c + 1)
                 prep_basis(c + 1)
-            main(c)
+            acc_first(c)
+        acc_second(NCH - 1)

@@ -81,7 +81,7 @@ def tile_bsplinebasis_t_kernel(tc, x, spline_coeffs, residual_weight, residual_b
         nc.vector.tensor_reduce(out=ssum[:], in_=sbraw[:], axis=AX.X, op=ALU.add)
         scale4 = const.tile([P, 4], F32)
         nc.vector.tensor_scalar(out=scale4[:], in0=ssum[:], scalar1=1.0 / I, scalar2=None, op0=ALU.mult)
-        scale_b = scale4[:].rearrange("p (u e) -> p u e", e=2).unsqueeze(1).to_broadcast([P, 2 * P, 2, 2])
+        scale_b = scale4[:].unsqueeze(1).to_broadcast([P, 2 * P, 4])
 
         cgp = setup.tile([P, NB, I, 4], BF16, align_bytes=64)
         cgn = setup.tile([P, NB, I, 4], BF16, align_bytes=64)
@@ -111,7 +111,7 @@ def tile_bsplinebasis_t_kernel(tc, x, spline_coeffs, residual_weight, residual_b
         nc.vector.quantize_mx(out=w_codes[:].bitcast(E4X4), scales=w_scl[:], in_=wg[:].rearrange("p i t -> p (i t)"))
         nc.vector.quantize_mx(out=c1_codes[:].bitcast(E4X4), scales=c1_scl[:], in_=cg1[:].rearrange("p i t -> p (i t)"))
 
-        xT = const.tile([P, B], BF16)
+        xT = const.tile([P, B], F32)
         a_nat = const.tile([P, NT, I], BF16)
 
         def prep_x(grp):
@@ -119,7 +119,8 @@ def tile_bsplinebasis_t_kernel(tc, x, spline_coeffs, residual_weight, residual_b
             for k in range(8):
                 nc.tensor.transpose(xt_ps[:, P * k:P * k + P], x_sb[:, 8 * grp + k, :], ident_b[:])
             nc.scalar.copy(out=xT[:, 1024 * grp:1024 * grp + 1024], in_=xt_ps[:])
-            nc.scalar.activation(out=a_nat[:, 8 * grp:8 * grp + 8, :], in_=x_sb[:, 8 * grp:8 * grp + 8, :], func=ACT.Abs)
+            nc.gpsimd.tensor_tensor(out=a_nat[:, 8 * grp:8 * grp + 8, :], in0=x_sb[:, 8 * grp:8 * grp + 8, :],
+                                    in1=x_sb[:, 8 * grp:8 * grp + 8, :], op=ALU.mult)
 
         q_tiles = {}
 
@@ -138,10 +139,8 @@ def tile_bsplinebasis_t_kernel(tc, x, spline_coeffs, residual_weight, residual_b
             for hf in range(2):
                 bank = banks[hf]
                 toks = slice(256 * hf, 256 * hf + 256)
-                nc.vector.tensor_tensor(out=gsq[:, toks, :].rearrange("p t (u e) -> p t u e", e=2),
-                                        in0=bank[:].bitcast(BF16).rearrange("p u (t e) -> p t u e", e=2),
-                                        in1=scale_b, op=ALU.mult)
                 nc.scalar.copy(out=gq[:, toks, :].bitcast(F32), in_=bank[:].rearrange("p u t -> p t u"))
+                nc.gpsimd.tensor_tensor(out=gsq[:, toks, :], in0=gq[:, toks, :], in1=scale_b, op=ALU.mult)
             q_tiles[c] = (gq, gsq)
 
         def quant_g(c):
@@ -161,7 +160,7 @@ def tile_bsplinebasis_t_kernel(tc, x, spline_coeffs, residual_weight, residual_b
             z = []
             for k in range(5):
                 zk = basis.tile([P, CT], F32, name="z%d" % k)
-                nc.gpsimd.tensor_scalar(out=zk[:], in0=ws, scalar1=-1.0 + H * (k + 1), scalar2=-1.0 + H * k,
+                nc.vector.tensor_scalar(out=zk[:], in0=ws, scalar1=-1.0 + H * (k + 1), scalar2=-1.0 + H * k,
                                         op0=ALU.min, op1=ALU.max)
                 z.append(zk)
             up = []
@@ -175,8 +174,7 @@ def tile_bsplinebasis_t_kernel(tc, x, spline_coeffs, residual_weight, residual_b
                 up.append(uk)
             planes = {-1: dn[0], 4: up[4]}
             for a in range(4):
-                eng = nc.vector if a < 2 else nc.gpsimd
-                eng.tensor_tensor(out=up[a][:], in0=up[a][:], in1=dn[a + 1][:], op=ALU.subtract)
+                nc.gpsimd.tensor_tensor(out=up[a][:], in0=up[a][:], in1=dn[a + 1][:], op=ALU.subtract)
                 planes[a] = up[a]
             plane_tiles[c] = planes
 

@@ -25,7 +25,7 @@ FLOPS = 2 * B * O * (I * NB + I)
 H = 0.4
 INV_H = 2.5
 ALPHA = math.sqrt(0.5 * INV_H)
-PIN = False
+PIN = True
 
 
 def tile_bsplinebasis_t_kernel(tc, x, spline_coeffs, residual_weight, residual_bias, scale_base, grad_out, out):
@@ -81,7 +81,7 @@ def tile_bsplinebasis_t_kernel(tc, x, spline_coeffs, residual_weight, residual_b
         nc.vector.tensor_reduce(out=ssum[:], in_=sbraw[:], axis=AX.X, op=ALU.add)
         scale4 = const.tile([P, 4], F32)
         nc.vector.tensor_scalar(out=scale4[:], in0=ssum[:], scalar1=1.0 / I, scalar2=None, op0=ALU.mult)
-        scale_b = scale4[:].unsqueeze(1).to_broadcast([P, 2 * P, 4])
+        scale_b = scale4[:].rearrange("p (u e) -> p u e", e=2).unsqueeze(1).to_broadcast([P, 2 * P, 2, 2])
 
         cgp = setup.tile([P, NB, I, 4], BF16, align_bytes=64)
         cgn = setup.tile([P, NB, I, 4], BF16, align_bytes=64)
@@ -111,7 +111,7 @@ def tile_bsplinebasis_t_kernel(tc, x, spline_coeffs, residual_weight, residual_b
         nc.vector.quantize_mx(out=w_codes[:].bitcast(E4X4), scales=w_scl[:], in_=wg[:].rearrange("p i t -> p (i t)"))
         nc.vector.quantize_mx(out=c1_codes[:].bitcast(E4X4), scales=c1_scl[:], in_=cg1[:].rearrange("p i t -> p (i t)"))
 
-        xT = const.tile([P, B], F32)
+        xT = const.tile([P, B], BF16)
         a_nat = const.tile([P, NT, I], BF16)
 
         def prep_x(grp):
@@ -119,12 +119,11 @@ def tile_bsplinebasis_t_kernel(tc, x, spline_coeffs, residual_weight, residual_b
             for k in range(8):
                 nc.tensor.transpose(xt_ps[:, P * k:P * k + P], x_sb[:, 8 * grp + k, :], ident_b[:])
             nc.scalar.copy(out=xT[:, 1024 * grp:1024 * grp + 1024], in_=xt_ps[:])
-            nc.gpsimd.tensor_tensor(out=a_nat[:, 8 * grp:8 * grp + 8, :], in0=x_sb[:, 8 * grp:8 * grp + 8, :],
-                                    in1=x_sb[:, 8 * grp:8 * grp + 8, :], op=ALU.mult)
+            nc.scalar.activation(out=a_nat[:, 8 * grp:8 * grp + 8, :], in_=x_sb[:, 8 * grp:8 * grp + 8, :], func=ACT.Abs)
 
         q_tiles = {}
 
-        def prep_g(c):
+        def tr_g(c):
             g_sb = g_tiles.pop(c)
             gq = gq_pool.tile([P, CT, 4], BF16, name="gq", align_bytes=64)
             gsq = gq_pool.tile([P, CT, 4], BF16, name="gsq", align_bytes=64)
@@ -136,47 +135,75 @@ def tile_bsplinebasis_t_kernel(tc, x, spline_coeffs, residual_weight, residual_b
                     for u in range(2):
                         nc.tensor.transpose(bank[:, u, P * k:P * k + P], gw[:, P * u:P * u + P], ident_f[:])
                 banks.append(bank)
-            for hf in range(2):
-                bank = banks[hf]
-                toks = slice(256 * hf, 256 * hf + 256)
-                nc.scalar.copy(out=gq[:, toks, :].bitcast(F32), in_=bank[:].rearrange("p u t -> p t u"))
-                nc.gpsimd.tensor_tensor(out=gsq[:, toks, :], in0=gq[:, toks, :], in1=scale_b, op=ALU.mult)
-            q_tiles[c] = (gq, gsq)
+            q_tiles[c] = {"gq": gq, "gsq": gsq, "banks": banks}
 
-        def quant_g(c):
-            gq, gsq = q_tiles.pop(c)
-            g_codes = gq_pool.tile([P, CT], U32, name="g_codes", align_bytes=64)
-            g_scl = gq_pool.tile([P, CT], U8, name="g_scl", align_bytes=64)
+        def copy_g(c):
+            q = q_tiles[c]
+            for hf in range(2):
+                toks = slice(256 * hf, 256 * hf + 256)
+                nc.scalar.copy(out=q["gq"][:, toks, :].bitcast(F32), in_=q["banks"][hf][:].rearrange("p u t -> p t u"))
+
+        def scale_g(c):
+            q = q_tiles[c]
+            for hf in range(2):
+                toks = slice(256 * hf, 256 * hf + 256)
+                nc.vector.tensor_tensor(out=q["gsq"][:, toks, :].rearrange("p t (u e) -> p t u e", e=2),
+                                        in0=q["banks"][hf][:].bitcast(BF16).rearrange("p u (t e) -> p t u e", e=2),
+                                        in1=scale_b, op=ALU.mult)
+
+        def quant_gs(c):
+            q = q_tiles[c]
             gs_codes = gq_pool.tile([P, CT], U32, name="gs_codes", align_bytes=64)
             gs_scl = gq_pool.tile([P, CT], U8, name="gs_scl", align_bytes=64)
-            nc.vector.quantize_mx(out=gs_codes[:].bitcast(E5X4), scales=gs_scl[:], in_=gsq[:].rearrange("p t k -> p (t k)"))
-            nc.vector.quantize_mx(out=g_codes[:].bitcast(E5X4), scales=g_scl[:], in_=gq[:].rearrange("p t k -> p (t k)"))
-            q_tiles[c] = (g_codes, g_scl, gs_codes, gs_scl)
+            nc.vector.quantize_mx(out=gs_codes[:].bitcast(E5X4), scales=gs_scl[:], in_=q["gsq"][:].rearrange("p t k -> p (t k)"))
+            q["gs"] = (gs_codes, gs_scl)
+
+        def quant_g(c):
+            q = q_tiles[c]
+            g_codes = gq_pool.tile([P, CT], U32, name="g_codes", align_bytes=64)
+            g_scl = gq_pool.tile([P, CT], U8, name="g_scl", align_bytes=64)
+            nc.vector.quantize_mx(out=g_codes[:].bitcast(E5X4), scales=g_scl[:], in_=q["gq"][:].rearrange("p t k -> p (t k)"))
+            q_tiles[c] = (g_codes, g_scl, q["gs"][0], q["gs"][1])
 
         plane_tiles = {}
+        z_tiles = {}
 
-        def prep_basis(c):
+        def zeta(c):
             ws = xT[:, CT * c:CT * c + CT]
             z = []
             for k in range(5):
                 zk = basis.tile([P, CT], F32, name="z%d" % k)
-                nc.vector.tensor_scalar(out=zk[:], in0=ws, scalar1=-1.0 + H * (k + 1), scalar2=-1.0 + H * k,
+                nc.gpsimd.tensor_scalar(out=zk[:], in0=ws, scalar1=-1.0 + H * (k + 1), scalar2=-1.0 + H * k,
                                         op0=ALU.min, op1=ALU.max)
                 z.append(zk)
-            up = []
-            dn = []
-            for k in range(5):
-                dk = basis.tile([P, CT], F32, name="dn%d" % k)
-                nc.scalar.activation(out=dk[:], in_=z[k][:], func=ACT.Square, scale=-INV_H * ALPHA, bias=(k - 1.5) * ALPHA)
-                dn.append(dk)
-                uk = basis.tile([P, CT], F32, name="up%d" % k)
-                nc.scalar.activation(out=uk[:], in_=z[k][:], func=ACT.Square, scale=INV_H * ALPHA, bias=(2.5 - k) * ALPHA)
-                up.append(uk)
-            planes = {-1: dn[0], 4: up[4]}
-            for a in range(4):
-                nc.gpsimd.tensor_tensor(out=up[a][:], in0=up[a][:], in1=dn[a + 1][:], op=ALU.subtract)
-                planes[a] = up[a]
-            plane_tiles[c] = planes
+            z_tiles[c] = z
+            plane_tiles[c] = {}
+
+        def square(c, kind, k):
+            z = z_tiles[c]
+            if kind == "up":
+                t = basis.tile([P, CT], F32, name="up%d" % k)
+                nc.scalar.activation(out=t[:], in_=z[k][:], func=ACT.Square, scale=INV_H * ALPHA, bias=(2.5 - k) * ALPHA)
+            else:
+                t = basis.tile([P, CT], F32, name="dn%d" % k)
+                nc.scalar.activation(out=t[:], in_=z[k][:], func=ACT.Square, scale=-INV_H * ALPHA, bias=(k - 1.5) * ALPHA)
+            plane_tiles[c][(kind, k)] = t
+
+        SQ_ORDER = [("up", 0), ("dn", 1), ("dn", 0), ("up", 1), ("dn", 2), ("up", 2), ("dn", 3), ("up", 3), ("dn", 4), ("up", 4)]
+
+        def squares(c, lo, hi):
+            for kind, k in SQ_ORDER[lo:hi]:
+                square(c, kind, k)
+
+        def step(c, a, eng):
+            pl = plane_tiles[c]
+            eng.tensor_tensor(out=pl[("up", a)][:], in0=pl[("up", a)][:], in1=pl[("dn", a + 1)][:], op=ALU.subtract)
+
+        def plane(c, a):
+            pl = plane_tiles[c]
+            if a == -1:
+                return pl[("dn", 0)]
+            return pl[("up", a)]
 
         def pos(j):
             return cp_codes[:, I * j:I * j + I].bitcast(E4X4), cp_scl[:, I * j:I * j + I]
@@ -194,39 +221,40 @@ def tile_bsplinebasis_t_kernel(tc, x, spline_coeffs, residual_weight, residual_b
         acc_tiles = {}
         pending = {}
 
+        e_banks = {}
+
         def mx_first(c):
             g_codes, g_scl, gs_codes, gs_scl = q_tiles[c]
-            planes = plane_tiles[c]
             e_r = group([(w_codes[:].bitcast(E4X4), w_scl[:])], g_codes, g_scl)
             e_c = group([pos(2), (c1_codes[:].bitcast(E4X4), c1_scl[:])], gs_codes, gs_scl)
             e_m = group([pos(2), neg2(1), pos(0)], gs_codes, gs_scl)
             e_0 = group([pos(3), neg2(2), pos(1)], gs_codes, gs_scl)
-            out_list = []
-            pr = prods.tile([P, CT], F32, name="pr")
-            nc.scalar.copy(out=pr[:], in_=e_r[:])
-            out_list.append(pr)
-            pr = prods.tile([P, CT], F32, name="pr")
-            nc.scalar.mul(out=pr[:], in_=e_c[:], mul=INV_H)
-            out_list.append(pr)
-            pr = prods.tile([P, CT], F32, name="pr")
-            nc.vector.scalar_tensor_tensor(out=pr[:], in0=planes[-1][:], scalar=-1.0, in1=e_m[:], op0=ALU.mult, op1=ALU.mult)
-            out_list.append(pr)
-            pr = prods.tile([P, CT], F32, name="pr")
-            nc.vector.scalar_tensor_tensor(out=pr[:], in0=planes[0][:], scalar=0.5 * INV_H, in1=e_0[:], op0=ALU.add, op1=ALU.mult)
-            out_list.append(pr)
-            pending[(c, 0)] = out_list
+            e_banks[c] = {"r": e_r, "c": e_c, -1: e_m, 0: e_0}
+            pending[(c, 0)] = []
+            pending[(c, 1)] = []
 
         def mx_second(c):
             g_codes, g_scl, gs_codes, gs_scl = q_tiles.pop(c)
-            planes = plane_tiles.pop(c)
-            banks = [group([pos(a + 3), neg2(a + 2), pos(a + 1)], gs_codes, gs_scl) for a in range(1, 5)]
-            out_list = []
             for a in range(1, 5):
-                pr = prods.tile([P, CT], F32, name="pr")
-                nc.vector.scalar_tensor_tensor(out=pr[:], in0=planes[a][:], scalar=(0.0 if a == 4 else 0.5 * INV_H), in1=banks[a - 1][:],
-                                               op0=ALU.add, op1=ALU.mult)
-                out_list.append(pr)
-            pending[(c, 1)] = out_list
+                e_banks[c][a] = group([pos(a + 3), neg2(a + 2), pos(a + 1)], gs_codes, gs_scl)
+
+        def copies(c):
+            pr = prods.tile([P, CT], F32, name="pr")
+            nc.scalar.copy(out=pr[:], in_=e_banks[c]["r"][:])
+            pending[(c, 0)].append(pr)
+            pr = prods.tile([P, CT], F32, name="pr")
+            nc.scalar.mul(out=pr[:], in_=e_banks[c]["c"][:], mul=INV_H)
+            pending[(c, 0)].append(pr)
+
+        def product(c, a):
+            pr = prods.tile([P, CT], F32, name="pr")
+            if a == -1:
+                nc.vector.scalar_tensor_tensor(out=pr[:], in0=plane(c, a)[:], scalar=-1.0, in1=e_banks[c][a][:],
+                                               op0=ALU.mult, op1=ALU.mult)
+            else:
+                nc.vector.scalar_tensor_tensor(out=pr[:], in0=plane(c, a)[:], scalar=(0.0 if a == 4 else 0.5 * INV_H),
+                                               in1=e_banks[c][a][:], op0=ALU.add, op1=ALU.mult)
+            pending[(c, 0 if a < 1 else 1)].append(pr)
 
         def acc_first(c):
             acc = ps_a.tile([P, CH, I], F32, name="acc")
@@ -246,6 +274,10 @@ def tile_bsplinebasis_t_kernel(tc, x, spline_coeffs, residual_weight, residual_b
                 for n in range(CH):
                     nc.tensor.matmul(out=acc[:, n, :], lhsT=pr[:, P * n:P * n + P], rhs=ident_f[:], is_transpose=True,
                                      start=False, stop=(idx == 3 and n == CH - 1))
+            acc_tiles[c] = (acc, accr)
+
+        def final(c):
+            acc, accr = acc_tiles.pop(c)
             tmp = work.tile([P, CH, I], F32, name="tmp")
             nc.vector.scalar_tensor_tensor(out=tmp[:], in0=a_nat[:, CH * c:CH * c + CH, :], scalar=1.0, in1=acc[:],
                                            op0=ALU.is_lt, op1=ALU.mult)
@@ -256,22 +288,50 @@ def tile_bsplinebasis_t_kernel(tc, x, spline_coeffs, residual_weight, residual_b
         if PIN:
             ctx.enter_context(tc.manual_schedule())
         prep_x(0)
-        prep_g(0)
-        prep_basis(0)
+        tr_g(0)
+        copy_g(0)
+        scale_g(0)
+        zeta(0)
+        squares(0, 0, 10)
+        quant_gs(0)
         quant_g(0)
+        step(0, 2, nc.gpsimd)
+        step(0, 3, nc.gpsimd)
         for c in range(NCH):
+            nxt = c + 1 < NCH
             if c + 2 < NCH:
                 load_g(c + 2)
             mx_first(c)
-            if c + 1 < NCH:
-                prep_g(c + 1)
-            if c % 2 == 0 and c // 2 + 1 < NT // 8:
-                prep_x(c // 2 + 1)
+            if nxt:
+                zeta(c + 1)
+            step(c, 0, nc.vector)
+            step(c, 1, nc.vector)
+            copies(c)
+            if nxt:
+                squares(c + 1, 0, 3)
+                tr_g(c + 1)
+            product(c, -1)
+            product(c, 0)
+            if nxt:
+                copy_g(c + 1)
+                scale_g(c + 1)
             if c > 0:
                 acc_second(c - 1)
+                final(c - 1)
             mx_second(c)
-            if c + 1 < NCH:
+            if nxt:
+                squares(c + 1, 3, 10)
+                step(c + 1, 2, nc.gpsimd)
+                step(c + 1, 3, nc.gpsimd)
+                quant_gs(c + 1)
+            product(c, 1)
+            product(c, 2)
+            if nxt:
                 quant_g(c + 1)
-                prep_basis(c + 1)
+            product(c, 3)
+            product(c, 4)
             acc_first(c)
+            if c % 2 == 0 and c // 2 + 1 < NT // 8:
+                prep_x(c // 2 + 1)
         acc_second(NCH - 1)
+        final(NCH - 1)

@@ -111,7 +111,7 @@ def tile_bsplinebasis_t_kernel(tc, x, spline_coeffs, residual_weight, residual_b
         nc.vector.quantize_mx(out=w_codes[:].bitcast(E4X4), scales=w_scl[:], in_=wg[:].rearrange("p i t -> p (i t)"))
         nc.vector.quantize_mx(out=c1_codes[:].bitcast(E4X4), scales=c1_scl[:], in_=cg1[:].rearrange("p i t -> p (i t)"))
 
-        xT = const.tile([P, B], BF16)
+        xT = const.tile([P, B], F32)
         a_nat = const.tile([P, NT, I], BF16)
 
         def prep_x(grp):
@@ -173,7 +173,8 @@ def tile_bsplinebasis_t_kernel(tc, x, spline_coeffs, residual_weight, residual_b
             z = []
             for k in range(5):
                 zk = basis.tile([P, CT], F32, name="z%d" % k)
-                nc.gpsimd.tensor_scalar(out=zk[:], in0=ws, scalar1=-1.0 + H * (k + 1), scalar2=-1.0 + H * k,
+                eng = nc.vector if k < 3 else nc.gpsimd
+                eng.tensor_scalar(out=zk[:], in0=ws, scalar1=-1.0 + H * (k + 1), scalar2=-1.0 + H * k,
                                         op0=ALU.min, op1=ALU.max)
                 z.append(zk)
             z_tiles[c] = z
@@ -295,8 +296,8 @@ def tile_bsplinebasis_t_kernel(tc, x, spline_coeffs, residual_weight, residual_b
         squares(0, 0, 10)
         quant_gs(0)
         quant_g(0)
-        step(0, 2, nc.gpsimd)
-        step(0, 3, nc.gpsimd)
+        for a in range(4):
+            step(0, a, nc.gpsimd)
         for c in range(NCH):
             nxt = c + 1 < NCH
             if c + 2 < NCH:
@@ -304,8 +305,6 @@ def tile_bsplinebasis_t_kernel(tc, x, spline_coeffs, residual_weight, residual_b
             mx_first(c)
             if nxt:
                 zeta(c + 1)
-            step(c, 0, nc.vector)
-            step(c, 1, nc.vector)
             copies(c)
             if nxt:
                 squares(c + 1, 0, 3)
@@ -321,8 +320,8 @@ def tile_bsplinebasis_t_kernel(tc, x, spline_coeffs, residual_weight, residual_b
             mx_second(c)
             if nxt:
                 squares(c + 1, 3, 10)
-                step(c + 1, 2, nc.gpsimd)
-                step(c + 1, 3, nc.gpsimd)
+                for a in range(4):
+                    step(c + 1, a, nc.gpsimd)
                 quant_gs(c + 1)
             product(c, 1)
             product(c, 2)

@@ -41,8 +41,9 @@ def tile_bsplinebasis_t_kernel(tc, x, spline_coeffs, residual_weight, residual_b
         gin = ctx.enter_context(tc.tile_pool(name="gin", bufs=3))
         gq_pool = ctx.enter_context(tc.tile_pool(name="gq", bufs=2))
         basis = ctx.enter_context(tc.tile_pool(name="basis", bufs=2))
+        zpool = ctx.enter_context(tc.tile_pool(name="zpool", bufs=1))
         work = ctx.enter_context(tc.tile_pool(name="work", bufs=2))
-        prods = ctx.enter_context(tc.tile_pool(name="prods", bufs=10))
+        prods = ctx.enter_context(tc.tile_pool(name="prods", bufs=12))
         ps_e = ctx.enter_context(tc.psum_pool(name="ps_e", bufs=4))
         ps_a = ctx.enter_context(tc.psum_pool(name="ps_a", bufs=1))
         ps_t = ctx.enter_context(tc.psum_pool(name="ps_t", bufs=2))
@@ -114,12 +115,17 @@ def tile_bsplinebasis_t_kernel(tc, x, spline_coeffs, residual_weight, residual_b
         xT = const.tile([P, B], F32)
         a_nat = const.tile([P, NT, I], BF16)
 
-        def prep_x(grp):
-            xt_ps = ps_t.tile([P, 8 * P], BF16, tag="tr")
-            for k in range(8):
-                nc.tensor.transpose(xt_ps[:, P * k:P * k + P], x_sb[:, 8 * grp + k, :], ident_b[:])
-            nc.scalar.copy(out=xT[:, 1024 * grp:1024 * grp + 1024], in_=xt_ps[:])
-            nc.scalar.activation(out=a_nat[:, 8 * grp:8 * grp + 8, :], in_=x_sb[:, 8 * grp:8 * grp + 8, :], func=ACT.Abs)
+        x_banks = {}
+
+        def tr_x(c):
+            xt_ps = ps_t.tile([P, CT], BF16, tag="tr")
+            for k in range(CH):
+                nc.tensor.transpose(xt_ps[:, P * k:P * k + P], x_sb[:, CH * c + k, :], ident_b[:])
+            x_banks[c] = xt_ps
+
+        def copy_x(c):
+            nc.scalar.copy(out=xT[:, CT * c:CT * c + CT], in_=x_banks.pop(c)[:])
+            nc.scalar.activation(out=a_nat[:, CH * c:CH * c + CH, :], in_=x_sb[:, CH * c:CH * c + CH, :], func=ACT.Abs)
 
         q_tiles = {}
 
@@ -172,7 +178,7 @@ def tile_bsplinebasis_t_kernel(tc, x, spline_coeffs, residual_weight, residual_b
             ws = xT[:, CT * c:CT * c + CT]
             z = []
             for k in range(5):
-                zk = basis.tile([P, CT], F32, name="z%d" % k)
+                zk = zpool.tile([P, CT], F32, name="z%d" % k)
                 eng = nc.vector if k < 3 else nc.gpsimd
                 eng.tensor_scalar(out=zk[:], in0=ws, scalar1=-1.0 + H * (k + 1), scalar2=-1.0 + H * k,
                                         op0=ALU.min, op1=ALU.max)
@@ -190,7 +196,7 @@ def tile_bsplinebasis_t_kernel(tc, x, spline_coeffs, residual_weight, residual_b
                 nc.scalar.activation(out=t[:], in_=z[k][:], func=ACT.Square, scale=-INV_H * ALPHA, bias=(k - 1.5) * ALPHA)
             plane_tiles[c][(kind, k)] = t
 
-        SQ_ORDER = [("up", 0), ("dn", 1), ("dn", 0), ("up", 1), ("dn", 2), ("up", 2), ("dn", 3), ("up", 3), ("dn", 4), ("up", 4)]
+        SQ_ORDER = [("dn", 0), ("up", 0), ("dn", 1), ("up", 1), ("dn", 2), ("up", 2), ("dn", 3), ("up", 3), ("dn", 4), ("up", 4)]
 
         def squares(c, lo, hi):
             for kind, k in SQ_ORDER[lo:hi]:
@@ -224,28 +230,26 @@ def tile_bsplinebasis_t_kernel(tc, x, spline_coeffs, residual_weight, residual_b
 
         e_banks = {}
 
-        def mx_first(c):
+        def mx(c, names):
             g_codes, g_scl, gs_codes, gs_scl = q_tiles[c]
-            e_r = group([(w_codes[:].bitcast(E4X4), w_scl[:])], g_codes, g_scl)
-            e_c = group([pos(2), (c1_codes[:].bitcast(E4X4), c1_scl[:])], gs_codes, gs_scl)
-            e_m = group([pos(2), neg2(1), pos(0)], gs_codes, gs_scl)
-            e_0 = group([pos(3), neg2(2), pos(1)], gs_codes, gs_scl)
-            e_banks[c] = {"r": e_r, "c": e_c, -1: e_m, 0: e_0}
-            pending[(c, 0)] = []
-            pending[(c, 1)] = []
-
-        def mx_second(c):
-            g_codes, g_scl, gs_codes, gs_scl = q_tiles.pop(c)
-            for a in range(1, 5):
-                e_banks[c][a] = group([pos(a + 3), neg2(a + 2), pos(a + 1)], gs_codes, gs_scl)
+            if c not in e_banks:
+                e_banks[c] = {}
+                pending[c] = {}
+            for a in names:
+                if a == "r":
+                    e_banks[c][a] = group([(w_codes[:].bitcast(E4X4), w_scl[:])], g_codes, g_scl)
+                elif a == "c":
+                    e_banks[c][a] = group([pos(2), (c1_codes[:].bitcast(E4X4), c1_scl[:])], gs_codes, gs_scl)
+                else:
+                    e_banks[c][a] = group([pos(a + 3), neg2(a + 2), pos(a + 1)], gs_codes, gs_scl)
 
         def copies(c):
             pr = prods.tile([P, CT], F32, name="pr")
-            nc.scalar.copy(out=pr[:], in_=e_banks[c]["r"][:])
-            pending[(c, 0)].append(pr)
-            pr = prods.tile([P, CT], F32, name="pr")
             nc.scalar.mul(out=pr[:], in_=e_banks[c]["c"][:], mul=INV_H)
-            pending[(c, 0)].append(pr)
+            pending[c]["c"] = pr
+            pr = prods.tile([P, CT], F32, name="pr")
+            nc.scalar.copy(out=pr[:], in_=e_banks[c]["r"][:])
+            pending[c]["r"] = pr
 
         def product(c, a):
             pr = prods.tile([P, CT], F32, name="pr")
@@ -255,27 +259,22 @@ def tile_bsplinebasis_t_kernel(tc, x, spline_coeffs, residual_weight, residual_b
             else:
                 nc.vector.scalar_tensor_tensor(out=pr[:], in0=plane(c, a)[:], scalar=(0.0 if a == 4 else 0.5 * INV_H),
                                                in1=e_banks[c][a][:], op0=ALU.add, op1=ALU.mult)
-            pending[(c, 0 if a < 1 else 1)].append(pr)
+            pending[c][a] = pr
 
-        def acc_first(c):
-            acc = ps_a.tile([P, CH, I], F32, name="acc")
-            accr = ps_a.tile([P, CH, I], F32, name="accr")
-            acc_tiles[c] = (acc, accr)
-            plist = pending.pop((c, 0))
-            for n in range(CH):
-                nc.tensor.transpose(accr[:, n, :], plist[0][:, P * n:P * n + P], ident_f[:])
-            for idx, pr in enumerate(plist[1:]):
+        def accumulate(c, names):
+            if c not in acc_tiles:
+                acc = ps_a.tile([P, CH, I], F32, name="acc")
+                accr = ps_a.tile([P, CH, I], F32, name="accr")
+                acc_tiles[c] = (acc, accr)
+            acc, accr = acc_tiles[c]
+            for a in names:
+                pr = pending[c].pop(a)
                 for n in range(CH):
-                    nc.tensor.matmul(out=acc[:, n, :], lhsT=pr[:, P * n:P * n + P], rhs=ident_f[:], is_transpose=True,
-                                     start=(idx == 0 and n == 0), stop=False)
-
-        def acc_second(c):
-            acc, accr = acc_tiles.pop(c)
-            for idx, pr in enumerate(pending.pop((c, 1))):
-                for n in range(CH):
-                    nc.tensor.matmul(out=acc[:, n, :], lhsT=pr[:, P * n:P * n + P], rhs=ident_f[:], is_transpose=True,
-                                     start=False, stop=(idx == 3 and n == CH - 1))
-            acc_tiles[c] = (acc, accr)
+                    if a == "r":
+                        nc.tensor.transpose(accr[:, n, :], pr[:, P * n:P * n + P], ident_f[:])
+                    else:
+                        nc.tensor.matmul(out=acc[:, n, :], lhsT=pr[:, P * n:P * n + P], rhs=ident_f[:], is_transpose=True,
+                                         start=(a == "c" and n == 0), stop=(a == 4 and n == CH - 1))
 
         def final(c):
             acc, accr = acc_tiles.pop(c)
@@ -288,7 +287,9 @@ def tile_bsplinebasis_t_kernel(tc, x, spline_coeffs, residual_weight, residual_b
 
         if PIN:
             ctx.enter_context(tc.manual_schedule())
-        prep_x(0)
+        for c in range(3):
+            tr_x(c)
+            copy_x(c)
         tr_g(0)
         copy_g(0)
         scale_g(0)
@@ -302,35 +303,43 @@ def tile_bsplinebasis_t_kernel(tc, x, spline_coeffs, residual_weight, residual_b
             nxt = c + 1 < NCH
             if c + 2 < NCH:
                 load_g(c + 2)
-            mx_first(c)
+            mx(c, ["c", "r", -1])
             if nxt:
                 zeta(c + 1)
             copies(c)
             if nxt:
-                squares(c + 1, 0, 3)
-                tr_g(c + 1)
+                squares(c + 1, 0, 5)
             product(c, -1)
-            product(c, 0)
+            if c > 0:
+                accumulate(c - 1, [2, 3, 4])
+                final(c - 1)
+            mx(c, [0, 1])
             if nxt:
+                step(c + 1, 0, nc.gpsimd)
+                step(c + 1, 1, nc.gpsimd)
+            product(c, 0)
+            product(c, 1)
+            if nxt:
+                tr_g(c + 1)
                 copy_g(c + 1)
                 scale_g(c + 1)
-            if c > 0:
-                acc_second(c - 1)
-                final(c - 1)
-            mx_second(c)
-            if nxt:
-                squares(c + 1, 3, 10)
-                for a in range(4):
-                    step(c + 1, a, nc.gpsimd)
-                quant_gs(c + 1)
-            product(c, 1)
+            mx(c, [2, 3])
             product(c, 2)
             if nxt:
-                quant_g(c + 1)
+                quant_gs(c + 1)
             product(c, 3)
+            if nxt:
+                squares(c + 1, 5, 10)
+                step(c + 1, 2, nc.gpsimd)
+                step(c + 1, 3, nc.gpsimd)
+            accumulate(c, ["c", "r", -1])
+            mx(c, [4])
+            if nxt:
+                quant_g(c + 1)
             product(c, 4)
-            acc_first(c)
-            if c % 2 == 0 and c // 2 + 1 < NT // 8:
-                prep_x(c // 2 + 1)
-        acc_second(NCH - 1)
+            accumulate(c, [0, 1])
+            if c + 3 < NCH:
+                tr_x(c + 3)
+                copy_x(c + 3)
+        accumulate(NCH - 1, [2, 3, 4])
         final(NCH - 1)

@@ -7,6 +7,7 @@ from concourse.masks import make_identity
 F32 = mybir.dt.float32
 BF16 = mybir.dt.bfloat16
 U32 = mybir.dt.uint32
+I32 = mybir.dt.int32
 U8 = mybir.dt.uint8
 E4X4 = mybir.dt.float8_e4m3fn_x4
 E5X4 = mybir.dt.float8_e5m2_x4
@@ -25,7 +26,6 @@ FLOPS = 2 * B * O * (I * NB + I)
 H = 0.4
 INV_H = 2.5
 ALPHA = math.sqrt(0.5 * INV_H)
-PIN = True
 
 
 def tile_bsplinebasis_t_kernel(tc, x, spline_coeffs, residual_weight, residual_bias, scale_base, grad_out, out):
@@ -40,13 +40,16 @@ def tile_bsplinebasis_t_kernel(tc, x, spline_coeffs, residual_weight, residual_b
         setup = ctx.enter_context(tc.tile_pool(name="setup", bufs=1))
         gin = ctx.enter_context(tc.tile_pool(name="gin", bufs=3))
         gq_pool = ctx.enter_context(tc.tile_pool(name="gq", bufs=2))
+        code_pool = ctx.enter_context(tc.tile_pool(name="codes", bufs=3))
         basis = ctx.enter_context(tc.tile_pool(name="basis", bufs=2))
-        zpool = ctx.enter_context(tc.tile_pool(name="zpool", bufs=1))
+        zpool = ctx.enter_context(tc.tile_pool(name="zpool", bufs=2))
         work = ctx.enter_context(tc.tile_pool(name="work", bufs=2))
         prods = ctx.enter_context(tc.tile_pool(name="prods", bufs=12))
         ps_e = ctx.enter_context(tc.psum_pool(name="ps_e", bufs=4))
         ps_a = ctx.enter_context(tc.psum_pool(name="ps_a", bufs=1))
         ps_t = ctx.enter_context(tc.psum_pool(name="ps_t", bufs=2))
+
+        ctx.enter_context(tc.manual_schedule())
 
         ident_f = const.tile([P, P], F32)
         make_identity(nc, ident_f[:])
@@ -54,29 +57,33 @@ def tile_bsplinebasis_t_kernel(tc, x, spline_coeffs, residual_weight, residual_b
         make_identity(nc, ident_b[:])
 
         sbraw = setup.tile([P, 4, I], BF16)
-        for u in range(2):
-            nc.sync.dma_start(out=sbraw[:, 2 * u:2 * u + 2, :],
-                              in_=scale_base[256 * u:256 * u + 256, :].rearrange("(q e) c -> q e c", e=2))
+        craw = setup.tile([P, 4, I * NB], BF16)
+        wraw = setup.tile([P, 4, I], BF16)
+        x_sb = const.tile([P, NT, I], BF16)
         g_tiles = {}
+
+        def load_halves(dst, src):
+            for u in range(2):
+                nc.sync.dma_start(out=dst[:, 2 * u:2 * u + 2, :],
+                                  in_=src[256 * u:256 * u + 256, :].rearrange("(q e) c -> q e c", e=2))
 
         def load_g(c):
             g_sb = gin.tile([P, CH, O], BF16, name="g_sb")
             nc.sync.dma_start(out=g_sb[:], in_=g_view[:, CH * c:CH * c + CH, :])
             g_tiles[c] = g_sb
 
+        def load_x(lo, hi):
+            nc.sync.dma_start(out=x_sb[:, lo:hi, :], in_=x_view[:, lo:hi, :])
+
+        load_halves(sbraw, scale_base)
         load_g(0)
-        craw = setup.tile([P, 4, I * NB], BF16)
-        for u in range(2):
-            nc.sync.dma_start(out=craw[:, 2 * u:2 * u + 2, :],
-                              in_=c_flat[256 * u:256 * u + 256, :].rearrange("(q e) c -> q e c", e=2))
-        wraw = setup.tile([P, 4, I], BF16)
-        for u in range(2):
-            nc.sync.dma_start(out=wraw[:, 2 * u:2 * u + 2, :],
-                              in_=residual_weight[256 * u:256 * u + 256, :].rearrange("(q e) c -> q e c", e=2))
-        x_sb = const.tile([P, NT, I], BF16)
-        nc.sync.dma_start(out=x_sb[:, 0:16, :], in_=x_view[:, 0:16, :])
-        nc.sync.dma_start(out=x_sb[:, 16:NT, :], in_=x_view[:, 16:NT, :])
+        load_x(0, CH)
+        load_halves(craw, c_flat)
+        load_halves(wraw, residual_weight)
         load_g(1)
+        load_x(CH, 16)
+        load_g(2)
+        load_x(16, NT)
 
         ssum = setup.tile([P, 4], F32)
         nc.vector.tensor_reduce(out=ssum[:], in_=sbraw[:], axis=AX.X, op=ALU.add)
@@ -91,31 +98,25 @@ def tile_bsplinebasis_t_kernel(tc, x, spline_coeffs, residual_weight, residual_b
         cp_scl = const.tile([P, NB * I], U8, align_bytes=64)
         cn_codes = const.tile([P, NB * I], U32, align_bytes=64)
         cn_scl = const.tile([P, NB * I], U8, align_bytes=64)
-        nc.vector.tensor_copy(out=cgp[:, 0:4], in_=c_perm[:, 0:4])
-        nc.scalar.mul(out=cgn[:, 0:4], in_=c_perm[:, 0:4], mul=-2.0)
-        nc.vector.tensor_copy(out=cgp[:, 4:8], in_=c_perm[:, 4:8])
-        nc.gpsimd.tensor_scalar(out=cgn[:, 4:8], in0=c_perm[:, 4:8], scalar1=-2.0, scalar2=0.0, op0=ALU.mult, op1=ALU.add)
         cg1 = setup.tile([P, I, 4], BF16, align_bytes=64)
-        nc.scalar.mul(out=cg1[:], in_=c_perm[:, 1], mul=-1.0)
         c1_codes = const.tile([P, I], U32, align_bytes=64)
         c1_scl = const.tile([P, I], U8, align_bytes=64)
         wg = setup.tile([P, I, 4], BF16, align_bytes=64)
-        nc.vector.tensor_copy(out=wg[:], in_=wraw[:].rearrange("p t i -> p i t"))
         w_codes = const.tile([P, I], U32, align_bytes=64)
         w_scl = const.tile([P, I], U8, align_bytes=64)
-        for hf in range(2):
-            cols = slice(512 * hf, 512 * hf + 512)
-            nc.vector.quantize_mx(out=cp_codes[:, cols].bitcast(E4X4), scales=cp_scl[:, cols],
-                                  in_=cgp[:, 4 * hf:4 * hf + 4].rearrange("p j i t -> p (j i t)"))
-            nc.vector.quantize_mx(out=cn_codes[:, cols].bitcast(E4X4), scales=cn_scl[:, cols],
-                                  in_=cgn[:, 4 * hf:4 * hf + 4].rearrange("p j i t -> p (j i t)"))
-        nc.vector.quantize_mx(out=w_codes[:].bitcast(E4X4), scales=w_scl[:], in_=wg[:].rearrange("p i t -> p (i t)"))
-        nc.vector.quantize_mx(out=c1_codes[:].bitcast(E4X4), scales=c1_scl[:], in_=cg1[:].rearrange("p i t -> p (i t)"))
 
-        xT = const.tile([P, B], F32)
+        def q_weights(codes, scl, src, lo, hi):
+            nc.vector.quantize_mx(out=codes[:, I * lo:I * hi].bitcast(E4X4), scales=scl[:, I * lo:I * hi],
+                                  in_=src[:, lo:hi].rearrange("p j i t -> p (j i t)"))
+
+        xT = const.tile([P, B], BF16)
         a_nat = const.tile([P, NT, I], BF16)
-
         x_banks = {}
+
+        def abs_x(lo, hi):
+            nc.vector.tensor_scalar(out=a_nat[:, lo:hi, :].rearrange("p n i -> p (n i)").bitcast(I32),
+                                    in0=x_sb[:, lo:hi, :].rearrange("p n i -> p (n i)").bitcast(I32),
+                                    scalar1=0x7FFF7FFF, scalar2=None, op0=ALU.bitwise_and)
 
         def tr_x(c):
             xt_ps = ps_t.tile([P, CT], BF16, tag="tr")
@@ -125,14 +126,12 @@ def tile_bsplinebasis_t_kernel(tc, x, spline_coeffs, residual_weight, residual_b
 
         def copy_x(c):
             nc.scalar.copy(out=xT[:, CT * c:CT * c + CT], in_=x_banks.pop(c)[:])
-            nc.scalar.activation(out=a_nat[:, CH * c:CH * c + CH, :], in_=x_sb[:, CH * c:CH * c + CH, :], func=ACT.Abs)
 
         q_tiles = {}
 
         def tr_g(c):
             g_sb = g_tiles.pop(c)
-            gq = gq_pool.tile([P, CT, 4], BF16, name="gq", align_bytes=64)
-            gsq = gq_pool.tile([P, CT, 4], BF16, name="gsq", align_bytes=64)
+            gboth = gq_pool.tile([P, 2, CT, 4], BF16, name="gboth", align_bytes=64)
             banks = []
             for hf in range(2):
                 bank = ps_t.tile([P, 2, 2 * P], F32, tag="tr")
@@ -141,50 +140,40 @@ def tile_bsplinebasis_t_kernel(tc, x, spline_coeffs, residual_weight, residual_b
                     for u in range(2):
                         nc.tensor.transpose(bank[:, u, P * k:P * k + P], gw[:, P * u:P * u + P], ident_f[:])
                 banks.append(bank)
-            q_tiles[c] = {"gq": gq, "gsq": gsq, "banks": banks}
+            q_tiles[c] = {"gboth": gboth, "banks": banks}
 
-        def copy_g(c):
+        def copy_g(c, hf):
             q = q_tiles[c]
-            for hf in range(2):
-                toks = slice(256 * hf, 256 * hf + 256)
-                nc.scalar.copy(out=q["gq"][:, toks, :].bitcast(F32), in_=q["banks"][hf][:].rearrange("p u t -> p t u"))
+            nc.scalar.copy(out=q["gboth"][:, 0, 256 * hf:256 * hf + 256, :].bitcast(F32),
+                           in_=q["banks"][hf][:].rearrange("p u t -> p t u"))
 
-        def scale_g(c):
+        def scale_g(c, hf):
             q = q_tiles[c]
-            for hf in range(2):
-                toks = slice(256 * hf, 256 * hf + 256)
-                nc.vector.tensor_tensor(out=q["gsq"][:, toks, :].rearrange("p t (u e) -> p t u e", e=2),
-                                        in0=q["banks"][hf][:].bitcast(BF16).rearrange("p u (t e) -> p t u e", e=2),
-                                        in1=scale_b, op=ALU.mult)
+            nc.vector.tensor_tensor(out=q["gboth"][:, 1, 256 * hf:256 * hf + 256, :].rearrange("p t (u e) -> p t u e", e=2),
+                                    in0=q["banks"][hf][:].bitcast(BF16).rearrange("p u (t e) -> p t u e", e=2),
+                                    in1=scale_b, op=ALU.mult)
 
-        def quant_gs(c):
+        def quant(c):
             q = q_tiles[c]
-            gs_codes = gq_pool.tile([P, CT], U32, name="gs_codes", align_bytes=64)
-            gs_scl = gq_pool.tile([P, CT], U8, name="gs_scl", align_bytes=64)
-            nc.vector.quantize_mx(out=gs_codes[:].bitcast(E5X4), scales=gs_scl[:], in_=q["gsq"][:].rearrange("p t k -> p (t k)"))
-            q["gs"] = (gs_codes, gs_scl)
-
-        def quant_g(c):
-            q = q_tiles[c]
-            g_codes = gq_pool.tile([P, CT], U32, name="g_codes", align_bytes=64)
-            g_scl = gq_pool.tile([P, CT], U8, name="g_scl", align_bytes=64)
-            nc.vector.quantize_mx(out=g_codes[:].bitcast(E5X4), scales=g_scl[:], in_=q["gq"][:].rearrange("p t k -> p (t k)"))
-            q_tiles[c] = (g_codes, g_scl, q["gs"][0], q["gs"][1])
+            codes = code_pool.tile([P, 2 * CT], U32, name="g_codes", align_bytes=64)
+            scl = code_pool.tile([P, 2 * CT], U8, name="g_scl", align_bytes=64)
+            nc.vector.quantize_mx(out=codes[:].bitcast(E5X4), scales=scl[:], in_=q["gboth"][:].rearrange("p s t k -> p (s t k)"))
+            q_tiles[c] = (codes, scl)
 
         plane_tiles = {}
         z_tiles = {}
 
-        def zeta(c):
+        def zeta(c, ks, eng=None):
+            eng = eng or nc.gpsimd
+            if c not in z_tiles:
+                z_tiles[c] = {}
+                plane_tiles[c] = {}
             ws = xT[:, CT * c:CT * c + CT]
-            z = []
-            for k in range(5):
+            for k in ks:
                 zk = zpool.tile([P, CT], F32, name="z%d" % k)
-                eng = nc.vector if k < 3 else nc.gpsimd
                 eng.tensor_scalar(out=zk[:], in0=ws, scalar1=-1.0 + H * (k + 1), scalar2=-1.0 + H * k,
                                         op0=ALU.min, op1=ALU.max)
-                z.append(zk)
-            z_tiles[c] = z
-            plane_tiles[c] = {}
+                z_tiles[c][k] = zk
 
         def square(c, kind, k):
             z = z_tiles[c]
@@ -202,7 +191,8 @@ def tile_bsplinebasis_t_kernel(tc, x, spline_coeffs, residual_weight, residual_b
             for kind, k in SQ_ORDER[lo:hi]:
                 square(c, kind, k)
 
-        def step(c, a, eng):
+        def step(c, a, eng=None):
+            eng = eng or nc.gpsimd
             pl = plane_tiles[c]
             eng.tensor_tensor(out=pl[("up", a)][:], in0=pl[("up", a)][:], in1=pl[("dn", a + 1)][:], op=ALU.subtract)
 
@@ -221,27 +211,26 @@ def tile_bsplinebasis_t_kernel(tc, x, spline_coeffs, residual_weight, residual_b
         def group(ops, rhs, rhs_scl):
             e_j = ps_e.tile([P, CT], F32, tag="e")
             for idx, (cd, sc) in enumerate(ops):
-                nc.tensor.matmul_mx(out=e_j[:], lhsT=cd, lhsT_scale=sc, rhs=rhs[:].bitcast(E5X4), rhs_scale=rhs_scl[:],
+                nc.tensor.matmul_mx(out=e_j[:], lhsT=cd, lhsT_scale=sc, rhs=rhs.bitcast(E5X4), rhs_scale=rhs_scl,
                                     start=(idx == 0), stop=(idx == len(ops) - 1))
             return e_j
 
         acc_tiles = {}
         pending = {}
-
         e_banks = {}
 
         def mx(c, names):
-            g_codes, g_scl, gs_codes, gs_scl = q_tiles[c]
+            codes, scl = q_tiles[c]
             if c not in e_banks:
                 e_banks[c] = {}
                 pending[c] = {}
             for a in names:
                 if a == "r":
-                    e_banks[c][a] = group([(w_codes[:].bitcast(E4X4), w_scl[:])], g_codes, g_scl)
+                    e_banks[c][a] = group([(w_codes[:].bitcast(E4X4), w_scl[:])], codes[:, 0:CT], scl[:, 0:CT])
                 elif a == "c":
-                    e_banks[c][a] = group([pos(2), (c1_codes[:].bitcast(E4X4), c1_scl[:])], gs_codes, gs_scl)
+                    e_banks[c][a] = group([pos(2), (c1_codes[:].bitcast(E4X4), c1_scl[:])], codes[:, CT:2 * CT], scl[:, CT:2 * CT])
                 else:
-                    e_banks[c][a] = group([pos(a + 3), neg2(a + 2), pos(a + 1)], gs_codes, gs_scl)
+                    e_banks[c][a] = group([pos(a + 3), neg2(a + 2), pos(a + 1)], codes[:, CT:2 * CT], scl[:, CT:2 * CT])
 
         def copies(c):
             pr = prods.tile([P, CT], F32, name="pr")
@@ -276,70 +265,114 @@ def tile_bsplinebasis_t_kernel(tc, x, spline_coeffs, residual_weight, residual_b
                         nc.tensor.matmul(out=acc[:, n, :], lhsT=pr[:, P * n:P * n + P], rhs=ident_f[:], is_transpose=True,
                                          start=(a == "c" and n == 0), stop=(a == 4 and n == CH - 1))
 
-        def final(c):
-            acc, accr = acc_tiles.pop(c)
+        tmp_tiles = {}
+
+        def final1(c):
+            acc, accr = acc_tiles[c]
             tmp = work.tile([P, CH, I], F32, name="tmp")
             nc.vector.scalar_tensor_tensor(out=tmp[:], in0=a_nat[:, CH * c:CH * c + CH, :], scalar=1.0, in1=acc[:],
                                            op0=ALU.is_lt, op1=ALU.mult)
+            tmp_tiles[c] = tmp
+
+        def final2(c):
+            acc, accr = acc_tiles.pop(c)
             o_sb = work.tile([P, CH, I], F32, name="o_sb")
-            nc.vector.tensor_tensor(out=o_sb[:], in0=tmp[:], in1=accr[:], op=ALU.add)
+            nc.vector.tensor_tensor(out=o_sb[:], in0=tmp_tiles.pop(c)[:], in1=accr[:], op=ALU.add)
             nc.sync.dma_start(out=o_view[:, CH * c:CH * c + CH, :], in_=o_sb[:])
 
-        if PIN:
-            ctx.enter_context(tc.manual_schedule())
-        for c in range(3):
-            tr_x(c)
-            copy_x(c)
+        tr_x(0)
+        copy_x(0)
+        zeta(0, range(5), nc.vector)
         tr_g(0)
-        copy_g(0)
-        scale_g(0)
-        zeta(0)
-        squares(0, 0, 10)
-        quant_gs(0)
-        quant_g(0)
-        for a in range(4):
-            step(0, a, nc.gpsimd)
-        for c in range(NCH):
-            nxt = c + 1 < NCH
-            if c + 2 < NCH:
-                load_g(c + 2)
-            mx(c, ["c", "r", -1])
-            if nxt:
-                zeta(c + 1)
-            copies(c)
-            if nxt:
-                squares(c + 1, 0, 5)
-            product(c, -1)
-            if c > 0:
-                accumulate(c - 1, [2, 3, 4])
-                final(c - 1)
-            mx(c, [0, 1])
-            if nxt:
-                step(c + 1, 0, nc.gpsimd)
-                step(c + 1, 1, nc.gpsimd)
-            product(c, 0)
-            product(c, 1)
-            if nxt:
-                tr_g(c + 1)
-                copy_g(c + 1)
-                scale_g(c + 1)
-            mx(c, [2, 3])
-            product(c, 2)
-            if nxt:
-                quant_gs(c + 1)
-            product(c, 3)
-            if nxt:
-                squares(c + 1, 5, 10)
-                step(c + 1, 2, nc.gpsimd)
-                step(c + 1, 3, nc.gpsimd)
-            accumulate(c, ["c", "r", -1])
-            mx(c, [4])
-            if nxt:
-                quant_g(c + 1)
-            product(c, 4)
-            accumulate(c, [0, 1])
-            if c + 3 < NCH:
-                tr_x(c + 3)
-                copy_x(c + 3)
+        scale_g(0, 0)
+        copy_g(0, 1)
+        squares(0, 0, 3)
+        copy_g(0, 0)
+        scale_g(0, 1)
+        squares(0, 3, 5)
+        nc.vector.tensor_copy(out=cgp[:, 0:4], in_=c_perm[:, 0:4])
+        nc.scalar.mul(out=cg1[:], in_=c_perm[:, 1], mul=-1.0)
+        nc.scalar.mul(out=cgn[:, 0:4], in_=c_perm[:, 0:4], mul=-2.0)
+        nc.scalar.copy(out=wg[:], in_=wraw[:].rearrange("p t i -> p i t"))
+        nc.scalar.mul(out=cgn[:, 4:8], in_=c_perm[:, 4:8], mul=-2.0)
+        squares(0, 5, 10)
+        quant(0)
+        q_weights(cp_codes, cp_scl, cgp, 0, 4)
+        nc.vector.quantize_mx(out=c1_codes[:].bitcast(E4X4), scales=c1_scl[:], in_=cg1[:].rearrange("p i t -> p (i t)"))
+        step(0, 0, nc.gpsimd)
+        q_weights(cn_codes, cn_scl, cgn, 0, 4)
+        nc.vector.quantize_mx(out=w_codes[:].bitcast(E4X4), scales=w_scl[:], in_=wg[:].rearrange("p i t -> p (i t)"))
+        step(0, 1, nc.gpsimd)
+        nc.vector.tensor_copy(out=cgp[:, 4:8], in_=c_perm[:, 4:8])
+        step(0, 2, nc.gpsimd)
+        step(0, 3, nc.gpsimd)
+        tr_x(1)
+        copy_x(1)
+        tr_x(2)
+        copy_x(2)
+        zeta(1, range(5), nc.gpsimd)
+
+        for i in range(NCH):
+            n1 = i + 1 < NCH
+            n2 = i + 2 < NCH
+            if i + 3 < NCH:
+                load_g(i + 3)
+            mx(i, ["c", "r", -1])
+            if i == 0:
+                q_weights(cp_codes, cp_scl, cgp, 4, 8)
+                tr_g(1)
+            elif n1:
+                quant(i + 1)
+            copies(i)
+            if n2:
+                zeta(i + 2, range(5))
+            product(i, -1)
+            if i == 0:
+                q_weights(cn_codes, cn_scl, cgn, 4, 8)
+                scale_g(1, 0)
+                copy_g(1, 1)
+                copy_g(1, 0)
+                scale_g(1, 1)
+            if i > 0:
+                accumulate(i - 1, [2, 3, 4])
+                final1(i - 1)
+            if n1:
+                squares(i + 1, 0, 6)
+            mx(i, [0, 1])
+            if n1:
+                step(i + 1, 0)
+                step(i + 1, 1)
+            product(i, 0)
+            if i > 0:
+                final2(i - 1)
+            product(i, 1)
+            if i == 0:
+                quant(1)
+            if n2:
+                tr_g(i + 2)
+                scale_g(i + 2, 0)
+                copy_g(i + 2, 1)
+            if n1:
+                squares(i + 1, 6, 7)
+            if n2:
+                copy_g(i + 2, 0)
+                scale_g(i + 2, 1)
+            if n1:
+                squares(i + 1, 7, 10)
+                step(i + 1, 2)
+                step(i + 1, 3)
+            mx(i, [2, 3])
+            product(i, 2)
+            product(i, 3)
+            accumulate(i, ["c", "r", -1])
+            mx(i, [4])
+            product(i, 4)
+            if i < 4:
+                abs_x(16 * i, 16 * i + 16)
+            accumulate(i, [0, 1])
+            if i + 3 < NCH:
+                tr_x(i + 3)
+                copy_x(i + 3)
         accumulate(NCH - 1, [2, 3, 4])
-        final(NCH - 1)
+        final1(NCH - 1)
+        final2(NCH - 1)

@@ -360,9 +360,10 @@ def tile_bsplinebasis_t_kernel(tc, x, spline_coeffs, residual_weight, residual_b
             if n1:
                 squares(i + 1, 7, 10)
                 step(i + 1, 2)
-                step(i + 1, 3)
             mx(i, [2, 3])
             product(i, 2)
+            if n1:
+                step(i + 1, 3, nc.vector)
             product(i, 3)
             accumulate(i, ["c", "r", -1])
             mx(i, [4])

@@ -359,17 +359,18 @@ def tile_bsplinebasis_t_kernel(tc, x, spline_coeffs, residual_weight, residual_b
                 scale_g(i + 2, 1)
             if n1:
                 squares(i + 1, 7, 10)
-                step(i + 1, 2)
             mx(i, [2, 3])
             product(i, 2)
             if n1:
-                step(i + 1, 3, nc.vector)
+                step(i + 1, 2, nc.vector)
             product(i, 3)
+            if n1:
+                step(i + 1, 3, nc.vector)
             accumulate(i, ["c", "r", -1])
             mx(i, [4])
             product(i, 4)
-            if i < 4:
-                abs_x(16 * i, 16 * i + 16)
+            if i % 4 == 0:
+                abs_x(4 * i, 4 * i + 16)
             accumulate(i, [0, 1])
             if i + 3 < NCH:
                 tr_x(i + 3)

@@ -76,12 +76,12 @@ def tile_bsplinebasis_t_kernel(tc, x, spline_coeffs, residual_weight, residual_b
             nc.sync.dma_start(out=x_sb[:, lo:hi, :], in_=x_view[:, lo:hi, :])
 
         load_halves(sbraw, scale_base)
+        load_x(0, 2 * CH)
         load_g(0)
-        load_x(0, CH)
         load_halves(craw, c_flat)
         load_halves(wraw, residual_weight)
         load_g(1)
-        load_x(CH, 16)
+        load_x(2 * CH, 16)
         load_g(2)
         load_x(16, NT)
 
@@ -118,8 +118,11 @@ def tile_bsplinebasis_t_kernel(tc, x, spline_coeffs, residual_weight, residual_b
                                     in0=x_sb[:, lo:hi, :].rearrange("p n i -> p (n i)").bitcast(I32),
                                     scalar1=0x7FFF7FFF, scalar2=None, op0=ALU.bitwise_and)
 
-        def tr_x(c):
-            xt_ps = ps_t.tile([P, CT], BF16, tag="tr")
+        def tr_x(c, early=False):
+            if early:
+                xt_ps = ps_e.tile([P, CT], BF16, tag="e")
+            else:
+                xt_ps = ps_t.tile([P, CT], BF16, tag="tr")
             for k in range(CH):
                 nc.tensor.transpose(xt_ps[:, P * k:P * k + P], x_sb[:, CH * c + k, :], ident_b[:])
             x_banks[c] = xt_ps
@@ -280,13 +283,17 @@ def tile_bsplinebasis_t_kernel(tc, x, spline_coeffs, residual_weight, residual_b
             nc.vector.tensor_tensor(out=o_sb[:], in0=tmp_tiles.pop(c)[:], in1=accr[:], op=ALU.add)
             nc.sync.dma_start(out=o_view[:, CH * c:CH * c + CH, :], in_=o_sb[:])
 
-        tr_x(0)
+        tr_x(0, True)
+        tr_x(1, True)
         copy_x(0)
         zeta(0, range(5), nc.vector)
+        squares(0, 0, 2)
+        copy_x(1)
+        zeta(1, range(3), nc.gpsimd)
         tr_g(0)
         scale_g(0, 0)
         copy_g(0, 1)
-        squares(0, 0, 3)
+        squares(0, 2, 3)
         copy_g(0, 0)
         scale_g(0, 1)
         squares(0, 3, 5)
@@ -294,23 +301,18 @@ def tile_bsplinebasis_t_kernel(tc, x, spline_coeffs, residual_weight, residual_b
         nc.scalar.mul(out=cg1[:], in_=c_perm[:, 1], mul=-1.0)
         nc.scalar.mul(out=cgn[:, 0:4], in_=c_perm[:, 0:4], mul=-2.0)
         nc.scalar.copy(out=wg[:], in_=wraw[:].rearrange("p t i -> p i t"))
-        nc.scalar.mul(out=cgn[:, 4:8], in_=c_perm[:, 4:8], mul=-2.0)
-        squares(0, 5, 10)
         quant(0)
         q_weights(cp_codes, cp_scl, cgp, 0, 4)
         nc.vector.quantize_mx(out=c1_codes[:].bitcast(E4X4), scales=c1_scl[:], in_=cg1[:].rearrange("p i t -> p (i t)"))
-        step(0, 0, nc.gpsimd)
+        step(0, 0, nc.vector)
         q_weights(cn_codes, cn_scl, cgn, 0, 4)
         nc.vector.quantize_mx(out=w_codes[:].bitcast(E4X4), scales=w_scl[:], in_=wg[:].rearrange("p i t -> p (i t)"))
-        step(0, 1, nc.gpsimd)
+        step(0, 1, nc.vector)
+        squares(0, 5, 7)
+        nc.scalar.mul(out=cgn[:, 4:8], in_=c_perm[:, 4:8], mul=-2.0)
+        squares(0, 7, 10)
         nc.vector.tensor_copy(out=cgp[:, 4:8], in_=c_perm[:, 4:8])
-        step(0, 2, nc.gpsimd)
-        step(0, 3, nc.gpsimd)
-        tr_x(1)
-        copy_x(1)
-        tr_x(2)
-        copy_x(2)
-        zeta(1, range(5), nc.gpsimd)
+        zeta(1, range(3, 5), nc.vector)
 
         for i in range(NCH):
             n1 = i + 1 < NCH
@@ -320,15 +322,17 @@ def tile_bsplinebasis_t_kernel(tc, x, spline_coeffs, residual_weight, residual_b
             mx(i, ["c", "r", -1])
             if i == 0:
                 q_weights(cp_codes, cp_scl, cgp, 4, 8)
+                step(0, 2, nc.vector)
                 tr_g(1)
             elif n1:
                 quant(i + 1)
             copies(i)
-            if n2:
-                zeta(i + 2, range(5))
+            if n1 and i > 0:
+                zeta(i + 1, range(5))
             product(i, -1)
             if i == 0:
                 q_weights(cn_codes, cn_scl, cgn, 4, 8)
+                step(0, 3, nc.vector)
                 scale_g(1, 0)
                 copy_g(1, 1)
                 copy_g(1, 0)
@@ -372,9 +376,9 @@ def tile_bsplinebasis_t_kernel(tc, x, spline_coeffs, residual_weight, residual_b
             if i % 4 == 0:
                 abs_x(4 * i, 4 * i + 16)
             accumulate(i, [0, 1])
-            if i + 3 < NCH:
-                tr_x(i + 3)
-                copy_x(i + 3)
+            if i + 2 < NCH:
+                tr_x(i + 2)
+                copy_x(i + 2)
         accumulate(NCH - 1, [2, 3, 4])
         final1(NCH - 1)
         final2(NCH - 1)

@@ -324,10 +324,9 @@ def tile_bsplinebasis_t_kernel(tc, x, spline_coeffs, residual_weight, residual_b
                 q_weights(cp_codes, cp_scl, cgp, 4, 8)
                 step(0, 2, nc.vector)
                 tr_g(1)
-            elif n1:
-                quant(i + 1)
             copies(i)
             if n1 and i > 0:
+                copy_x(i + 1)
                 zeta(i + 1, range(5))
             product(i, -1)
             if i == 0:
@@ -341,11 +340,8 @@ def tile_bsplinebasis_t_kernel(tc, x, spline_coeffs, residual_weight, residual_b
                 accumulate(i - 1, [2, 3, 4])
                 final1(i - 1)
             if n1:
-                squares(i + 1, 0, 6)
+                squares(i + 1, 0, 3)
             mx(i, [0, 1])
-            if n1:
-                step(i + 1, 0)
-                step(i + 1, 1)
             product(i, 0)
             if i > 0:
                 final2(i - 1)
@@ -357,28 +353,30 @@ def tile_bsplinebasis_t_kernel(tc, x, spline_coeffs, residual_weight, residual_b
                 scale_g(i + 2, 0)
                 copy_g(i + 2, 1)
             if n1:
-                squares(i + 1, 6, 7)
+                squares(i + 1, 3, 4)
             if n2:
                 copy_g(i + 2, 0)
                 scale_g(i + 2, 1)
             if n1:
-                squares(i + 1, 7, 10)
+                squares(i + 1, 4, 10)
+                step(i + 1, 0)
+                step(i + 1, 1)
             mx(i, [2, 3])
             product(i, 2)
-            if n1:
-                step(i + 1, 2, nc.vector)
             product(i, 3)
-            if n1:
-                step(i + 1, 3, nc.vector)
             accumulate(i, ["c", "r", -1])
             mx(i, [4])
             product(i, 4)
+            if n1:
+                step(i + 1, 2, nc.vector)
+                step(i + 1, 3, nc.vector)
+            if n2:
+                quant(i + 2)
             if i % 4 == 0:
                 abs_x(4 * i, 4 * i + 16)
             accumulate(i, [0, 1])
             if i + 2 < NCH:
                 tr_x(i + 2)
-                copy_x(i + 2)
         accumulate(NCH - 1, [2, 3, 4])
         final1(NCH - 1)
         final2(NCH - 1)

@@ -253,6 +253,10 @@ def tile_bsplinebasis_t_kernel(tc, x, spline_coeffs, residual_weight, residual_b
                                                in1=e_banks[c][a][:], op0=ALU.add, op1=ALU.mult)
             pending[c][a] = pr
 
+        def join(c, a, b):
+            pa = pending[c][a]
+            nc.vector.tensor_tensor(out=pa[:], in0=pa[:], in1=pending[c].pop(b)[:], op=ALU.add)
+
         def accumulate(c, names):
             if c not in acc_tiles:
                 acc = ps_a.tile([P, CH, I], F32, name="acc")
@@ -337,7 +341,7 @@ def tile_bsplinebasis_t_kernel(tc, x, spline_coeffs, residual_weight, residual_b
                 copy_g(1, 0)
                 scale_g(1, 1)
             if i > 0:
-                accumulate(i - 1, [2, 3, 4])
+                accumulate(i - 1, [2, 4])
                 final1(i - 1)
             if n1:
                 squares(i + 1, 0, 3)
@@ -367,6 +371,7 @@ def tile_bsplinebasis_t_kernel(tc, x, spline_coeffs, residual_weight, residual_b
             accumulate(i, ["c", "r", -1])
             mx(i, [4])
             product(i, 4)
+            join(i, 2, 3)
             if n1:
                 step(i + 1, 2, nc.vector)
                 step(i + 1, 3, nc.vector)
@@ -377,6 +382,6 @@ def tile_bsplinebasis_t_kernel(tc, x, spline_coeffs, residual_weight, residual_b
             accumulate(i, [0, 1])
             if i + 2 < NCH:
                 tr_x(i + 2)
-        accumulate(NCH - 1, [2, 3, 4])
+        accumulate(NCH - 1, [2, 4])
         final1(NCH - 1)
         final2(NCH - 1)

@@ -257,7 +257,7 @@ def tile_bsplinebasis_t_kernel(tc, x, spline_coeffs, residual_weight, residual_b
             pa = pending[c][a]
             nc.vector.tensor_tensor(out=pa[:], in0=pa[:], in1=pending[c].pop(b)[:], op=ALU.add)
 
-        def accumulate(c, names):
+        def accumulate(c, names, first=False, last=False):
             if c not in acc_tiles:
                 acc = ps_a.tile([P, CH, I], F32, name="acc")
                 accr = ps_a.tile([P, CH, I], F32, name="accr")
@@ -270,7 +270,7 @@ def tile_bsplinebasis_t_kernel(tc, x, spline_coeffs, residual_weight, residual_b
                         nc.tensor.transpose(accr[:, n, :], pr[:, P * n:P * n + P], ident_f[:])
                     else:
                         nc.tensor.matmul(out=acc[:, n, :], lhsT=pr[:, P * n:P * n + P], rhs=ident_f[:], is_transpose=True,
-                                         start=(a == "c" and n == 0), stop=(a == 4 and n == CH - 1))
+                                         start=(first and a == names[0] and n == 0), stop=(last and a == names[-1] and n == CH - 1))
 
         tmp_tiles = {}
 
@@ -329,6 +329,7 @@ def tile_bsplinebasis_t_kernel(tc, x, spline_coeffs, residual_weight, residual_b
                 step(0, 2, nc.vector)
                 tr_g(1)
             copies(i)
+            nc.scalar.activation(out=a_nat[:, CH * i:CH * i + CH, :], in_=x_sb[:, CH * i:CH * i + CH, :], func=ACT.Abs)
             if n1 and i > 0:
                 copy_x(i + 1)
                 zeta(i + 1, range(5))
@@ -341,7 +342,7 @@ def tile_bsplinebasis_t_kernel(tc, x, spline_coeffs, residual_weight, residual_b
                 copy_g(1, 0)
                 scale_g(1, 1)
             if i > 0:
-                accumulate(i - 1, [2, 4])
+                accumulate(i - 1, [4, 2], last=True)
                 final1(i - 1)
             if n1:
                 squares(i + 1, 0, 3)
@@ -368,7 +369,7 @@ def tile_bsplinebasis_t_kernel(tc, x, spline_coeffs, residual_weight, residual_b
             mx(i, [2, 3])
             product(i, 2)
             product(i, 3)
-            accumulate(i, ["c", "r", -1])
+            accumulate(i, ["c", "r", -1], first=True)
             mx(i, [4])
             product(i, 4)
             join(i, 2, 3)
@@ -377,11 +378,9 @@ def tile_bsplinebasis_t_kernel(tc, x, spline_coeffs, residual_weight, residual_b
                 step(i + 1, 3, nc.vector)
             if n2:
                 quant(i + 2)
-            if i % 4 == 0:
-                abs_x(4 * i, 4 * i + 16)
             accumulate(i, [0, 1])
             if i + 2 < NCH:
                 tr_x(i + 2)
-        accumulate(NCH - 1, [2, 4])
+        accumulate(NCH - 1, [4, 2], last=True)
         final1(NCH - 1)
         final2(NCH - 1)

from contextlib import ExitStack
import math

import concourse.mybir as mybir
from concourse.masks import make_identity

F32 = mybir.dt.float32
BF16 = mybir.dt.bfloat16
U32 = mybir.dt.uint32
I32 = mybir.dt.int32
U8 = mybir.dt.uint8
E4X4 = mybir.dt.float8_e4m3fn_x4
E5X4 = mybir.dt.float8_e5m2_x4
ALU = mybir.AluOpType
ACT = mybir.ActivationFunctionType
AX = mybir.AxisListType

P = 128
B, I, O, NB = 8192, 128, 512, 8
NT = B // P
CH = 4
CT = CH * P
NCH = NT // CH
FLOPS = 2 * B * O * (I * NB + I)

H = 0.4
INV_H = 2.5
ALPHA = math.sqrt(0.5 * INV_H)


def tile_bsplinebasis_t_kernel(tc, x, spline_coeffs, residual_weight, residual_bias, scale_base, grad_out, out):
    nc = tc.nc
    g_view = grad_out.rearrange("(p n) o -> p n o", n=NT)
    x_view = x.rearrange("(p n) i -> p n i", n=NT)
    o_view = out.rearrange("(p n) i -> p n i", n=NT)
    c_flat = spline_coeffs.rearrange("o i j -> o (i j)")

    with ExitStack() as ctx:
        const = ctx.enter_context(tc.tile_pool(name="const", bufs=1))
        setup = ctx.enter_context(tc.tile_pool(name="setup", bufs=1))
        gin = ctx.enter_context(tc.tile_pool(name="gin", bufs=3))
        gq_pool = ctx.enter_context(tc.tile_pool(name="gq", bufs=2))
        code_pool = ctx.enter_context(tc.tile_pool(name="codes", bufs=3))
        basis = ctx.enter_context(tc.tile_pool(name="basis", bufs=2))
        zpool = ctx.enter_context(tc.tile_pool(name="zpool", bufs=2))
        work = ctx.enter_context(tc.tile_pool(name="work", bufs=2))
        prods = ctx.enter_context(tc.tile_pool(name="prods", bufs=12))
        ps_e = ctx.enter_context(tc.psum_pool(name="ps_e", bufs=4))
        ps_a = ctx.enter_context(tc.psum_pool(name="ps_a", bufs=1))
        ps_t = ctx.enter_context(tc.psum_pool(name="ps_t", bufs=2))

        ctx.enter_context(tc.manual_schedule())

        ident_f = const.tile([P, P], F32)
        make_identity(nc, ident_f[:])
        ident_b = const.tile([P, P], BF16)
        make_identity(nc, ident_b[:])

        sbraw = setup.tile([P, 4, I], BF16)
        craw = setup.tile([P, 4, I * NB], BF16)
        wraw = setup.tile([P, 4, I], BF16)
        x_sb = const.tile([P, NT, I], BF16)
        g_tiles = {}

        def load_halves(dst, src):
            for u in range(2):
                nc.sync.dma_start(out=dst[:, 2 * u:2 * u + 2, :],
                                  in_=src[256 * u:256 * u + 256, :].rearrange("(q e) c -> q e c", e=2))

        def load_g(c):
            g_sb = gin.tile([P, CH, O], BF16, name="g_sb")
            nc.sync.dma_start(out=g_sb[:], in_=g_view[:, CH * c:CH * c + CH, :])
            g_tiles[c] = g_sb

        def load_x(lo, hi):
            nc.sync.dma_start(out=x_sb[:, lo:hi, :], in_=x_view[:, lo:hi, :])

        load_halves(sbraw, scale_base)
        load_x(0, 2 * CH)
        load_g(0)
        load_halves(craw, c_flat)
        load_halves(wraw, residual_weight)
        load_g(1)
        load_x(2 * CH, 16)
        load_g(2)
        load_x(16, NT)

        ssum = setup.tile([P, 4], F32)
        nc.vector.tensor_reduce(out=ssum[:], in_=sbraw[:], axis=AX.X, op=ALU.add)
        scale4 = const.tile([P, 4], F32)
        nc.vector.tensor_scalar(out=scale4[:], in0=ssum[:], scalar1=1.0 / I, scalar2=None, op0=ALU.mult)
        scale_b = scale4[:].rearrange("p (u e) -> p u e", e=2).unsqueeze(1).to_broadcast([P, 2 * P, 2, 2])

        cgp = setup.tile([P, NB, I, 4], BF16, align_bytes=64)
        cgn = setup.tile([P, NB, I, 4], BF16, align_bytes=64)
        c_perm = craw[:].rearrange("p t (i j) -> p j i t", j=NB)
        cp_codes = const.tile([P, NB * I], U32, align_bytes=64)
        cp_scl = const.tile([P, NB * I], U8, align_bytes=64)
        cn_codes = const.tile([P, NB * I], U32, align_bytes=64)
        cn_scl = const.tile([P, NB * I], U8, align_bytes=64)
        cg1 = setup.tile([P, I, 4], BF16, align_bytes=64)
        c1_codes = const.tile([P, I], U32, align_bytes=64)
        c1_scl = const.tile([P, I], U8, align_bytes=64)
        wg = setup.tile([P, I, 4], BF16, align_bytes=64)
        w_codes = const.tile([P, I], U32, align_bytes=64)
        w_scl = const.tile([P, I], U8, align_bytes=64)

        def q_weights(codes, scl, src, lo, hi):
            nc.vector.quantize_mx(out=codes[:, I * lo:I * hi].bitcast(E4X4), scales=scl[:, I * lo:I * hi],
                                  in_=src[:, lo:hi].rearrange("p j i t -> p (j i t)"))

        xT = const.tile([P, B], BF16)
        a_nat = const.tile([P, NT, I], BF16)
        x_banks = {}

        def abs_x(lo, hi):
            nc.vector.tensor_scalar(out=a_nat[:, lo:hi, :].rearrange("p n i -> p (n i)").bitcast(I32),
                                    in0=x_sb[:, lo:hi, :].rearrange("p n i -> p (n i)").bitcast(I32),
                                    scalar1=0x7FFF7FFF, scalar2=None, op0=ALU.bitwise_and)

        def tr_x(c, early=False):
            if early:
                xt_ps = ps_e.tile([P, CT], BF16, tag="e")
            else:
                xt_ps = ps_t.tile([P, CT], BF16, tag="tr")
            for k in range(CH):
                nc.tensor.transpose(xt_ps[:, P * k:P * k + P], x_sb[:, CH * c + k, :], ident_b[:])
            x_banks[c] = xt_ps

        def copy_x(c):
            nc.scalar.copy(out=xT[:, CT * c:CT * c + CT], in_=x_banks.pop(c)[:])

        q_tiles = {}

        def tr_g(c):
            g_sb = g_tiles.pop(c)
            gboth = gq_pool.tile([P, 2, CT, 4], BF16, name="gboth", align_bytes=64)
            banks = []
            for hf in range(2):
                bank = ps_t.tile([P, 2, 2 * P], F32, tag="tr")
                for k in range(2):
                    gw = g_sb[:, 2 * hf + k, :].bitcast(F32)
                    for u in range(2):
                        nc.tensor.transpose(bank[:, u, P * k:P * k + P], gw[:, P * u:P * u + P], ident_f[:])
                banks.append(bank)
            q_tiles[c] = {"gboth": gboth, "banks": banks}

        def copy_g(c, hf):
            q = q_tiles[c]
            nc.scalar.copy(out=q["gboth"][:, 0, 256 * hf:256 * hf + 256, :].bitcast(F32),
                           in_=q["banks"][hf][:].rearrange("p u t -> p t u"))

        def scale_g(c, hf):
            q = q_tiles[c]
            nc.vector.tensor_tensor(out=q["gboth"][:, 1, 256 * hf:256 * hf + 256, :].rearrange("p t (u e) -> p t u e", e=2),
                                    in0=q["banks"][hf][:].bitcast(BF16).rearrange("p u (t e) -> p t u e", e=2),
                                    in1=scale_b, op=ALU.mult)

        def quant(c):
            q = q_tiles[c]
            codes = code_pool.tile([P, 2 * CT], U32, name="g_codes", align_bytes=64)
            scl = code_pool.tile([P, 2 * CT], U8, name="g_scl", align_bytes=64)
            nc.vector.quantize_mx(out=codes[:].bitcast(E5X4), scales=scl[:], in_=q["gboth"][:].rearrange("p s t k -> p (s t k)"))
            q_tiles[c] = (codes, scl)

        plane_tiles = {}
        z_tiles = {}

        def zeta(c, ks, eng=None):
            eng = eng or nc.gpsimd
            if c not in z_tiles:
                z_tiles[c] = {}
                plane_tiles[c] = {}
            ws = xT[:, CT * c:CT * c + CT]
            for k in ks:
                zk = zpool.tile([P, CT], F32, name="z%d" % k)
                eng.tensor_scalar(out=zk[:], in0=ws, scalar1=-1.0 + H * (k + 1), scalar2=-1.0 + H * k,
                                        op0=ALU.min, op1=ALU.max)
                z_tiles[c][k] = zk

        def square(c, kind, k):
            z = z_tiles[c]
            if kind == "up":
                t = basis.tile([P, CT], F32, name="up%d" % k)
                nc.scalar.activation(out=t[:], in_=z[k][:], func=ACT.Square, scale=INV_H * ALPHA, bias=(2.5 - k) * ALPHA)
            else:
                t = basis.tile([P, CT], F32, name="dn%d" % k)
                nc.scalar.activation(out=t[:], in_=z[k][:], func=ACT.Square, scale=-INV_H * ALPHA, bias=(k - 1.5) * ALPHA)
            plane_tiles[c][(kind, k)] = t

        SQ_ORDER = [("dn", 0), ("up", 0), ("dn", 1), ("up", 1), ("dn", 2), ("up", 2), ("dn", 3), ("up", 3), ("dn", 4), ("up", 4)]

        def squares(c, lo, hi):
            for kind, k in SQ_ORDER[lo:hi]:
                square(c, kind, k)

        def step(c, a, eng=None):
            eng = eng or nc.gpsimd
            pl = plane_tiles[c]
            eng.tensor_tensor(out=pl[("up", a)][:], in0=pl[("up", a)][:], in1=pl[("dn", a + 1)][:], op=ALU.subtract)

        def plane(c, a):
            pl = plane_tiles[c]
            if a == -1:
                return pl[("dn", 0)]
            return pl[("up", a)]

        def pos(j):
            return cp_codes[:, I * j:I * j + I].bitcast(E4X4), cp_scl[:, I * j:I * j + I]

        def neg2(j):
            return cn_codes[:, I * j:I * j + I].bitcast(E4X4), cn_scl[:, I * j:I * j + I]

        def group(ops, rhs, rhs_scl):
            e_j = ps_e.tile([P, CT], F32, tag="e")
            for idx, (cd, sc) in enumerate(ops):
                nc.tensor.matmul_mx(out=e_j[:], lhsT=cd, lhsT_scale=sc, rhs=rhs.bitcast(E5X4), rhs_scale=rhs_scl,
                                    start=(idx == 0), stop=(idx == len(ops) - 1))
            return e_j

        acc_tiles = {}
        pending = {}
        e_banks = {}

        def mx(c, names):
            codes, scl = q_tiles[c]
            if c not in e_banks:
                e_banks[c] = {}
                pending[c] = {}
            for a in names:
                if a == "r":
                    e_banks[c][a] = group([(w_codes[:].bitcast(E4X4), w_scl[:])], codes[:, 0:CT], scl[:, 0:CT])
                elif a == "c":
                    e_banks[c][a] = group([pos(2), (c1_codes[:].bitcast(E4X4), c1_scl[:])], codes[:, CT:2 * CT], scl[:, CT:2 * CT])
                else:
                    e_banks[c][a] = group([pos(a + 3), neg2(a + 2), pos(a + 1)], codes[:, CT:2 * CT], scl[:, CT:2 * CT])

        def copies(c):
            pr = prods.tile([P, CT], F32, name="pr")
            nc.scalar.mul(out=pr[:], in_=e_banks[c]["c"][:], mul=INV_H)
            pending[c]["c"] = pr
            pr = prods.tile([P, CT], F32, name="pr")
            nc.scalar.copy(out=pr[:], in_=e_banks[c]["r"][:])
            pending[c]["r"] = pr

        def product(c, a):
            pr = prods.tile([P, CT], F32, name="pr")
            if a == -1:
                nc.vector.scalar_tensor_tensor(out=pr[:], in0=plane(c, a)[:], scalar=-1.0, in1=e_banks[c][a][:],
                                               op0=ALU.mult, op1=ALU.mult)
            else:
                nc.vector.scalar_tensor_tensor(out=pr[:], in0=plane(c, a)[:], scalar=(0.0 if a == 4 else 0.5 * INV_H),
                                               in1=e_banks[c][a][:], op0=ALU.add, op1=ALU.mult)
            pending[c][a] = pr

        def join(c, a, b):
            pa = pending[c][a]
            nc.vector.tensor_tensor(out=pa[:], in0=pa[:], in1=pending[c].pop(b)[:], op=ALU.add)

        def accumulate(c, names, first=False, last=False):
            if c not in acc_tiles:
                acc = ps_a.tile([P, CH, I], F32, name="acc")
                accr = ps_a.tile([P, CH, I], F32, name="accr")
                acc_tiles[c] = (acc, accr)
            acc, accr = acc_tiles[c]
            for a in names:
                pr = pending[c].pop(a)
                for n in range(CH):
                    if a == "r":
                        nc.tensor.transpose(accr[:, n, :], pr[:, P * n:P * n + P], ident_f[:])
                    else:
                        nc.tensor.matmul(out=acc[:, n, :], lhsT=pr[:, P * n:P * n + P], rhs=ident_f[:], is_transpose=True,
                                         start=(first and a == names[0] and n == 0), stop=(last and a == names[-1] and n == CH - 1))

        tmp_tiles = {}

        def final1(c):
            acc, accr = acc_tiles[c]
            tmp = work.tile([P, CH, I], F32, name="tmp")
            nc.vector.scalar_tensor_tensor(out=tmp[:], in0=a_nat[:, CH * c:CH * c + CH, :], scalar=1.0, in1=acc[:],
                                           op0=ALU.is_lt, op1=ALU.mult)
            tmp_tiles[c] = tmp

        def final2(c):
            acc, accr = acc_tiles.pop(c)
            o_sb = work.tile([P, CH, I], F32, name="o_sb")
            nc.vector.tensor_tensor(out=o_sb[:], in0=tmp_tiles.pop(c)[:], in1=accr[:], op=ALU.add)
            nc.sync.dma_start(out=o_view[:, CH * c:CH * c + CH, :], in_=o_sb[:])

        tr_x(0, True)
        tr_x(1, True)
        copy_x(0)
        zeta(0, range(5), nc.vector)
        squares(0, 0, 2)
        copy_x(1)
        zeta(1, range(3), nc.gpsimd)
        tr_g(0)
        scale_g(0, 0)
        copy_g(0, 1)
        squares(0, 2, 3)
        copy_g(0, 0)
        scale_g(0, 1)
        squares(0, 3, 5)
        nc.vector.tensor_copy(out=cgp[:, 0:4], in_=c_perm[:, 0:4])
        nc.scalar.mul(out=cg1[:], in_=c_perm[:, 1], mul=-1.0)
        nc.scalar.mul(out=cgn[:, 0:4], in_=c_perm[:, 0:4], mul=-2.0)
        nc.scalar.copy(out=wg[:], in_=wraw[:].rearrange("p t i -> p i t"))
        quant(0)
        q_weights(cp_codes, cp_scl, cgp, 0, 4)
        nc.vector.quantize_mx(out=c1_codes[:].bitcast(E4X4), scales=c1_scl[:], in_=cg1[:].rearrange("p i t -> p (i t)"))
        step(0, 0, nc.vector)
        q_weights(cn_codes, cn_scl, cgn, 0, 4)
        nc.vector.quantize_mx(out=w_codes[:].bitcast(E4X4), scales=w_scl[:], in_=wg[:].rearrange("p i t -> p (i t)"))
        step(0, 1, nc.vector)
        squares(0, 5, 7)
        nc.scalar.mul(out=cgn[:, 4:8], in_=c_perm[:, 4:8], mul=-2.0)
        squares(0, 7, 10)
        nc.vector.tensor_copy(out=cgp[:, 4:8], in_=c_perm[:, 4:8])
        zeta(1, range(3, 5), nc.vector)

        for i in range(NCH):
            n1 = i + 1 < NCH
            n2 = i + 2 < NCH
            if i + 3 < NCH:
                load_g(i + 3)
            mx(i, ["c", "r", -1])
            if i == 0:
                q_weights(cp_codes, cp_scl, cgp, 4, 8)
                step(0, 2, nc.vector)
                tr_g(1)
            copies(i)
            nc.scalar.activation(out=a_nat[:, CH * i:CH * i + CH, :], in_=x_sb[:, CH * i:CH * i + CH, :], func=ACT.Abs)
            if n1 and i > 0:
                copy_x(i + 1)
                zeta(i + 1, range(5))
            product(i, -1)
            if i == 0:
                q_weights(cn_codes, cn_scl, cgn, 4, 8)
                step(0, 3, nc.vector)
                scale_g(1, 0)
                copy_g(1, 1)
                copy_g(1, 0)
                scale_g(1, 1)
            if i > 0:
                accumulate(i - 1, [4, 2], last=True)
                final1(i - 1)
            if n1:
                squares(i + 1, 0, 3)
            mx(i, [0, 1])
            product(i, 0)
            if i > 0:
                final2(i - 1)
            product(i, 1)
            if i == 0:
                quant(1)
            if n2:
                tr_g(i + 2)
                scale_g(i + 2, 0)
                copy_g(i + 2, 1)
            if n1:
                squares(i + 1, 3, 4)
            if n2:
                copy_g(i + 2, 0)
                scale_g(i + 2, 1)
            if n1:
                squares(i + 1, 4, 10)
                step(i + 1, 0)
                step(i + 1, 1)
            mx(i, [2, 3])
            product(i, 2)
            product(i, 3)
            accumulate(i, ["c", "r", -1], first=True)
            mx(i, [4])
            product(i, 4)
            join(i, 2, 3)
            if n1:
                step(i + 1, 2, nc.vector)
                step(i + 1, 3, nc.vector)
            if n2:
                quant(i + 2)
            accumulate(i, [0, 1])
            if i + 2 < NCH:
                tr_x(i + 2)
        accumulate(NCH - 1, [4, 2], last=True)
        final1(NCH - 1)
        final2(NCH - 1)
